import numpy as np
import ml_dtypes


def mxq(x, axis, fmt="e4m3"):
    dtype, down = {"e4m3": (ml_dtypes.float8_e4m3fn, 7), "e5m2": (ml_dtypes.float8_e5m2, 14)}[fmt]
    v = np.moveaxis(np.asarray(x, np.float32).astype(ml_dtypes.bfloat16).astype(np.float64), axis, -1)
    blocks = v.reshape(v.shape[:-1] + (-1, 32))
    amax = np.abs(blocks).max(-1, keepdims=True)
    byte = np.maximum(np.where(amax > 0, np.frexp(amax)[1] - 1 + 127, 0) - down, 1)
    scale = np.exp2(byte - 127.0)
    codes = (blocks / scale).astype(np.float32).astype(dtype).astype(np.float64)
    return np.moveaxis((codes * scale).reshape(v.shape), -1, axis)


WIDE = False


def mx_kscale(k):
    if not WIDE:
        return np.ones(k)
    levels = np.array([10, -10, 5, -5, 0])
    a = np.random.permutation(np.resize(levels, k // 512 * 4)).reshape(k // 512, 4)
    idx = np.arange(k)
    return np.exp2(a[idx // 512, idx % 128 // 32])


BF16 = ml_dtypes.bfloat16


def bf(x):
    return np.asarray(x, np.float32).astype(BF16)


def f64(x):
    return np.asarray(x).astype(np.float64)


E2M1 = np.array([0.0, 0.5, 1.0, 1.5, 2.0, 3.0, 4.0, 6.0, -0.0, -0.5, -1.0, -1.5, -2.0, -3.0, -4.0, -6.0])


def pack_weight(w, fmt):
    k, n = w.shape
    w = f64(bf(w)).reshape(k // 32, 32, n)
    amax = np.abs(w).max(1)
    if fmt == "e4m3":
        byte = np.frexp(amax)[1] - 1 + 127 - 7
    else:
        mant, ex = np.frexp(amax / 6.0)
        byte = np.where(mant > 0.5, ex, ex - 1) + 127
    byte = np.clip(np.where(amax > 0, byte, 1), 1, 254)
    scaled = (w * np.exp2(127.0 - byte)[:, None, :]).reshape(k, n).astype(np.float32)
    by_word = np.ascontiguousarray(scaled.reshape(k // 512, 128, 4, n).transpose(0, 1, 3, 2))
    if fmt == "e4m3":
        words = by_word.astype(ml_dtypes.float8_e4m3fn).view(np.uint8)
    else:
        c = by_word.astype(ml_dtypes.float4_e2m1fn).view(np.uint8) & 0xF
        words = c[..., 0::2] | (c[..., 1::2] << 4)
    return np.ascontiguousarray(words), np.ascontiguousarray(byte.astype(np.uint8).reshape(k // 512, 16, n))


def unpack_weight(words, scales, fmt):
    g, p, n, _ = words.shape
    if fmt == "e4m3":
        vals = np.ascontiguousarray(words).view(ml_dtypes.float8_e4m3fn).astype(np.float64)
    else:
        nib = np.empty((g, p, n, 4), np.uint8)
        nib[..., 0::2] = words & 0xF
        nib[..., 1::2] = words >> 4
        vals = E2M1[nib]
    vals = vals * np.repeat(np.exp2(scales.astype(np.float64) - 127.0), 8, axis=1)[..., None]
    return vals.transpose(0, 1, 3, 2).reshape(g * 512, n)


B, N, D = 64, 8, 512
NT = 100
FMT = "e4m3"


def erf(v):
    c = np.clip(v, -6.0, 6.0)
    q = 2.0 * c * c
    acc = np.ones_like(c)
    for n in range(NT, 0, -1):
        acc = 1.0 + acc * q / (2 * n + 1)
    return 2.0 / np.sqrt(np.pi) * c * np.exp(-c * c) * acc


def gelu_erf(v):
    return 0.5 * v * (1.0 + erf(v / np.sqrt(2.0)))


def setup_inputs():
    s = mx_kscale(2 * D)[:D]
    s2 = np.concatenate([s, s])
    x = bf(np.random.standard_normal((B, N, D)) * s)
    W1_words, W1_scales = pack_weight(np.random.standard_normal((2 * D, 2 * D)) / np.sqrt(2 * D) / s2[:, None], FMT)
    b1 = bf(np.random.standard_normal(2 * D) * 0.5)
    W2_words, W2_scales = pack_weight(np.random.standard_normal((2 * D, D)) / np.sqrt(2 * D), FMT)
    b2 = bf(np.random.standard_normal(D) * 0.3)
    return {"x": x,
            "W1_words": W1_words,
            "W1_scales": W1_scales,
            "b1": b1,
            "W2_words": W2_words,
            "W2_scales": W2_scales,
            "b2": b2}


def reference(x, W1_words, W1_scales, b1, W2_words, W2_scales, b2):
    x, b1, b2 = f64(x), f64(b1), f64(b2)
    W1 = unpack_weight(W1_words, W1_scales, FMT)
    W2 = unpack_weight(W2_words, W2_scales, FMT)
    ii, jj = np.tril_indices(N)
    cat = np.concatenate([x[:, ii, :], x[:, jj, :]], axis=-1)
    h = gelu_erf((mxq(cat, 2, "e4m3") @ W1) + b1)
    pt = (mxq(h, 2, "e4m3") @ W2) + b2
    p = np.zeros((B, N, N, D))
    p[:, ii, jj, :] = pt
    mask = np.triu(np.ones((N, N), dtype=bool), 1)
    w = np.sqrt(np.sum(p * p, axis=-1))
    w = np.where(mask[None, :, :], -1e9, w)
    e = np.exp(w - w.max(-1, keepdims=True))
    w = (e / e.sum(-1, keepdims=True))[..., None]
    return np.sum(w * p, axis=2)

@@ -1,0 +1,306 @@
+from contextlib import ExitStack
+
+import concourse.mybir as mybir
+from concourse.masks import make_identity
+
+F32 = mybir.dt.float32
+BF16 = mybir.dt.bfloat16
+I32 = mybir.dt.int32
+U32 = mybir.dt.uint32
+U8 = mybir.dt.uint8
+FP8X4 = mybir.dt.float8_e4m3fn_x4
+ALU = mybir.AluOpType
+ACT = mybir.ActivationFunctionType
+AX = mybir.AxisListType
+
+P = 128
+BATCH = 64
+POSITIONS = 8
+D = 512
+HIDDEN = 1024
+HALVES = HIDDEN // D
+PACK = 4
+PAIRS = POSITIONS * (POSITIONS + 1) // 2
+WRAP_BLOCK = POSITIONS - 1
+GPSIMD_FROM = 6
+FLOPS = 2 * BATCH * PAIRS * (2 * D * HIDDEN + HIDDEN * D)
+
+
+def tile_lpair_kernel(tc, x, W1_words, W1_scales, b1, W2_words, W2_scales, b2, out):
+    nc = tc.nc
+    with ExitStack() as ctx:
+        keep = ctx.enter_context(tc.tile_pool(name="keep", bufs=1))
+        grp = ctx.enter_context(tc.tile_pool(name="grp", bufs=2))
+        work = ctx.enter_context(tc.tile_pool(name="work", bufs=3))
+        ps_first = ctx.enter_context(tc.psum_pool(name="ps_first", bufs=3))
+        ps_turn = ctx.enter_context(tc.psum_pool(name="ps_turn", bufs=3))
+        ps_second = ctx.enter_context(tc.psum_pool(name="ps_second", bufs=2))
+
+        x_sb = keep.tile([P, 4, D], BF16)
+        w1_words = keep.tile([P, 2, HIDDEN], U32, align_bytes=64)
+        w1_scales = keep.tile([P, 2, HIDDEN], U8, align_bytes=64)
+        w2_words = keep.tile([P, 2, D], U32, align_bytes=64)
+        w2_scales = keep.tile([P, 2, D], U8, align_bytes=64)
+        b1_all = keep.tile([P, HIDDEN], BF16)
+        b2_all = keep.tile([P, D], BF16)
+
+        nc.vector.memset(w1_scales[:].bitcast(I32), 0)
+        nc.vector.memset(w2_scales[:].bitcast(I32), 0)
+
+        nc.sync.dma_start(out=x_sb[:], in_=x.rearrange("(a c) i d -> (c i) a d", a=4))
+        for q in range(4):
+            nc.sync.dma_start(
+                out=w1_scales[32 * q : 32 * q + 4, :, :].bitcast(I32),
+                in_=W1_scales[:, 4 * q : 4 * q + 4, :].rearrange("g r n -> r g n").bitcast(I32),
+            )
+        for g in range(2):
+            nc.sync.dma_start(
+                out=w1_words[:, g, :].bitcast(I32),
+                in_=W1_words[g].rearrange("p n t -> p (n t)").bitcast(I32),
+            )
+        for q in range(4):
+            nc.sync.dma_start(
+                out=w2_scales[32 * q : 32 * q + 4, :, :].bitcast(I32),
+                in_=W2_scales[:, 4 * q : 4 * q + 4, :].rearrange("g r n -> r g n").bitcast(I32),
+            )
+        for g in range(2):
+            nc.sync.dma_start(
+                out=w2_words[:, g, :].bitcast(I32),
+                in_=W2_words[g].rearrange("p n t -> p (n t)").bitcast(I32),
+            )
+        nc.scalar.dma_start(out=b1_all[:], in_=b1.partition_broadcast(P))
+        nc.scalar.dma_start(out=b2_all[:], in_=b2.partition_broadcast(P))
+
+        ident = keep.tile([P, P], F32)
+        make_identity(nc, ident[:])
+        half = keep.tile([P, POSITIONS + 1], F32)
+        nc.vector.memset(half[:], 0.5)
+
+        x_grouped = keep.tile([P, POSITIONS, BATCH, PACK], BF16, align_bytes=64)
+        x_grouped_words = x_grouped[:].rearrange("p i b t -> p i (b t)").bitcast(F32).rearrange(
+            "p i (b u) -> p i b u", u=2
+        )
+        x_words = x_sb[:].bitcast(F32)
+        rows_b = BATCH // 4
+        for a in range(4):
+            x_turned = ps_turn.tile([P, 2, P], F32, tag="turned")
+            for u in range(2):
+                nc.tensor.transpose(x_turned[:, u, :], x_words[:, a, u : D // 2 : 2], ident[:])
+            nc.vector.tensor_copy(
+                out=x_grouped_words[:, :, rows_b * a : rows_b * (a + 1), :],
+                in_=x_turned[:].rearrange("p u (c i) -> p i c u", i=POSITIONS),
+            )
+        xq_words = keep.tile([P, (POSITIONS + 1) * BATCH], U32, align_bytes=64)
+        xq_scales = keep.tile([P, (POSITIONS + 1) * BATCH], U8, align_bytes=64)
+        x_flat = x_grouped[:].rearrange("p i b t -> p (i b t)")
+        nc.vector.quantize_mx(
+            out=xq_words[:, 0 : POSITIONS * BATCH].bitcast(FP8X4),
+            scales=xq_scales[:, 0 : POSITIONS * BATCH],
+            in_=x_flat,
+        )
+        nc.vector.quantize_mx(
+            out=xq_words[:, POSITIONS * BATCH :].bitcast(FP8X4),
+            scales=xq_scales[:, POSITIONS * BATCH :],
+            in_=x_flat[:, 0 : BATCH * PACK],
+        )
+
+        tiles = []
+        columns_of = {}
+        for sg in (3, 2, 1, 0):
+            blocks = list(range(2 * sg + 1)) + [WRAP_BLOCK]
+            columns_of[sg] = len(blocks)
+            for c, jb in enumerate(blocks):
+                tiles.append((sg, c, jb))
+        n_tiles = len(tiles)
+
+        p_all = keep.tile([P, n_tiles, D], F32)
+        first_half = {}
+        norm2 = {}
+        pre = {}
+        hq = {}
+        second = {}
+
+        def x_slice(block):
+            cols = slice(BATCH * block, BATCH * block + P)
+            return xq_words[:, cols].bitcast(FP8X4), xq_scales[:, cols]
+
+        def prepare_group(sg):
+            lhsT, lhsT_scale = x_slice(2 * sg)
+            a_b1 = grp.tile([P, HALVES, PACK, P], F32, tag="a_b1")
+            for h in range(HALVES):
+                cols = slice(D * h, D * (h + 1))
+                acc = ps_first.tile([P, D], F32, tag="first")
+                nc.tensor.matmul_mx(
+                    out=acc[:], lhsT=lhsT, lhsT_scale=lhsT_scale,
+                    rhs=w1_words[:, 0, cols].bitcast(FP8X4), rhs_scale=w1_scales[:, 0, cols],
+                    start=True, stop=True,
+                )
+                nc.vector.tensor_tensor(
+                    out=a_b1[:, h, :, :],
+                    in0=acc[:].rearrange("r (p t) -> r t p", t=PACK),
+                    in1=b1_all[:, cols].rearrange("r (p t) -> r t p", t=PACK),
+                    op=ALU.add,
+                )
+            first_half[sg] = a_b1
+            norm2[sg] = grp.tile([P, columns_of[sg]], F32, tag="norm2", name="norm2")
+
+        def first_matmul(k):
+            sg, c, jb = tiles[k]
+            lhsT, lhsT_scale = x_slice(jb)
+            h_pre = work.tile([P, HALVES, PACK, P], F32, tag="h_pre")
+            for h in range(HALVES):
+                cols = slice(D * h, D * (h + 1))
+                acc = ps_first.tile([P, D], F32, tag="first")
+                nc.tensor.matmul_mx(
+                    out=acc[:], lhsT=lhsT, lhsT_scale=lhsT_scale,
+                    rhs=w1_words[:, 1, cols].bitcast(FP8X4), rhs_scale=w1_scales[:, 1, cols],
+                    start=True, stop=True,
+                )
+                nc.vector.tensor_tensor(
+                    out=h_pre[:, h, :, :],
+                    in0=acc[:].rearrange("r (p t) -> r t p", t=PACK),
+                    in1=first_half[sg][:, h, :, :],
+                    op=ALU.add,
+                )
+            pre[k] = h_pre
+
+        def turn_and_gelu(k):
+            h_grouped = work.tile([P, HALVES, P, PACK], BF16, tag="h_grouped", align_bytes=64)
+            for h in range(HALVES):
+                turned = ps_turn.tile([P, PACK, P], F32, tag="turned")
+                for t in range(PACK):
+                    nc.tensor.transpose(turned[:, t, :], pre[k][:, h, t, :], ident[:])
+                nc.scalar.activation(
+                    out=h_grouped[:, h, :, :],
+                    in_=turned[:].rearrange("p t r -> p r t"),
+                    func=ACT.Gelu,
+                )
+            pre[k] = h_grouped
+
+        def quantise(k):
+            words = work.tile([P, HALVES * P], U32, tag="hq_words", align_bytes=64)
+            scales = work.tile([P, HALVES * P], U8, tag="hq_scales", align_bytes=64)
+            nc.vector.quantize_mx(
+                out=words[:].bitcast(FP8X4), scales=scales[:],
+                in_=pre[k][:].rearrange("p h r t -> p (h r t)"),
+            )
+            hq[k] = (words, scales)
+
+        def second_matmul(k):
+            words, scales = hq[k]
+            acc = ps_second.tile([P, D], F32, tag="second")
+            for h in range(HALVES):
+                rows = slice(P * h, P * (h + 1))
+                nc.tensor.matmul_mx(
+                    out=acc[:], lhsT=words[:, rows].bitcast(FP8X4), lhsT_scale=scales[:, rows],
+                    rhs=w2_words[:, h, :].bitcast(FP8X4), rhs_scale=w2_scales[:, h, :],
+                    start=(h == 0), stop=(h == HALVES - 1),
+                )
+            second[k] = acc
+
+        def add_b2(k):
+            nc.vector.tensor_tensor(out=p_all[:, k, :], in0=second[k][:], in1=b2_all[:], op=ALU.add)
+
+        def square(k):
+            sg, c, jb = tiles[k]
+            squares = work.tile([P, D], BF16, tag="squares")
+            nc.scalar.activation(
+                out=squares[:], in_=p_all[:, k, :], func=ACT.Square, accum_out=norm2[sg][:, c : c + 1]
+            )
+
+        norm_of = {}
+        tanh_of = {}
+        weight_of = {}
+
+        def norms(sg):
+            n = columns_of[sg]
+            norm = grp.tile([P, n], F32, tag="norm")
+            nc.gpsimd.tensor_tensor(out=norm[:], in0=norm2[sg][:], in1=half[:, 0:n], op=ALU.pow)
+            norm_of[sg] = norm
+
+        def shifted_tanh(sg):
+            n = columns_of[sg]
+            wrap = n - 1
+            norm = norm_of[sg]
+            nc.vector.tensor_copy(out=norm[0:BATCH, wrap : wrap + 1], in_=norm[0:BATCH, 0:1])
+            top = grp.tile([P, 1], F32, tag="top")
+            nc.vector.reduce_max(out=top[:], in_=norm[:], axis=AX.X)
+            shift = grp.tile([P, 1], F32, tag="shift")
+            nc.vector.tensor_scalar(shift[:], top[:], -0.5, None, ALU.mult)
+            th = grp.tile([P, n], F32, tag="th")
+            nc.scalar.activation(out=th[:], in_=norm[:], func=ACT.Tanh, bias=shift[:], scale=0.5)
+            tanh_of[sg] = th
+
+        def weights(sg):
+            n = columns_of[sg]
+            wrap = n - 1
+            th = tanh_of[sg]
+            num = grp.tile([P, n], F32, tag="num")
+            nc.vector.tensor_scalar(num[:], th[:], 1.0, None, ALU.add)
+            nc.vector.memset(num[0:BATCH, wrap : wrap + 1], 0.0)
+            den = grp.tile([P, n], F32, tag="den")
+            nc.vector.tensor_scalar(den[:], th[:], -1.0, 1.0, ALU.mult, ALU.add)
+            nc.vector.reciprocal(den[:], den[:])
+            e = grp.tile([P, n], F32, tag="e")
+            total = grp.tile([P, 1], F32, tag="total")
+            nc.vector.scalar_tensor_tensor(
+                out=e[:], in0=num[:], scalar=1.0, in1=den[:], op0=ALU.mult, op1=ALU.mult, accum_out=total[:]
+            )
+            nc.vector.reciprocal(total[:], total[:])
+            weight = grp.tile([P, n], F32, tag="weight")
+            nc.vector.tensor_scalar(weight[:], e[:], total[:], None, ALU.mult)
+            weight_of[sg] = weight
+
+        def pool_and_store(sg, k_first):
+            n = columns_of[sg]
+            weight = weight_of[sg]
+            pooled = grp.tile([P, D], F32, tag="pooled")
+            if n >= GPSIMD_FROM:
+                nc.gpsimd.tensor_scalar(pooled[:], p_all[:, k_first, :], weight[:, 0:1], 0.0, ALU.mult, ALU.add)
+                for c in range(1, n):
+                    term = work.tile([P, D], F32, tag="term")
+                    nc.gpsimd.tensor_scalar(
+                        term[:], p_all[:, k_first + c, :], weight[:, c : c + 1], 0.0, ALU.mult, ALU.add
+                    )
+                    nc.gpsimd.tensor_tensor(out=pooled[:], in0=pooled[:], in1=term[:], op=ALU.add)
+            else:
+                nc.vector.tensor_scalar(pooled[:], p_all[:, k_first, :], weight[:, 0:1], None, ALU.mult)
+                for c in range(1, n):
+                    nc.vector.scalar_tensor_tensor(
+                        out=pooled[:], in0=p_all[:, k_first + c, :], scalar=weight[:, c : c + 1], in1=pooled[:],
+                        op0=ALU.mult, op1=ALU.add,
+                    )
+            for s in range(2):
+                nc.sync.dma_start(out=out[:, 2 * sg + s, :], in_=pooled[BATCH * s : BATCH * (s + 1), :])
+
+        first_tile = {}
+        squares_done = {}
+        for k, (sg, c, jb) in enumerate(tiles):
+            if c == 0:
+                first_tile[sg] = k
+            squares_done[sg] = k + 4
+
+        prepare_group(tiles[0][0])
+        for step in range(n_tiles + 7):
+            if 0 <= step - 2 < n_tiles:
+                quantise(step - 2)
+            if 0 <= step - 3 < n_tiles:
+                add_b2(step - 3)
+            if 0 <= step - 4 < n_tiles:
+                square(step - 4)
+            for sg in columns_of:
+                if step == squares_done[sg]:
+                    norms(sg)
+                if step == squares_done[sg] + 1:
+                    shifted_tanh(sg)
+                if step == squares_done[sg] + 2:
+                    weights(sg)
+                    pool_and_store(sg, first_tile[sg])
+            if step < n_tiles:
+                first_matmul(step)
+            if step + 1 < n_tiles and tiles[step + 1][1] == 0:
+                prepare_group(tiles[step + 1][0])
+            if 0 <= step - 1 < n_tiles:
+                turn_and_gelu(step - 1)
+            if 0 <= step - 2 < n_tiles:
+                second_matmul(step - 2)

@@ -22,7 +22,6 @@ HALVES = HIDDEN // D
 PACK = 4
 PAIRS = POSITIONS * (POSITIONS + 1) // 2
 WRAP_BLOCK = POSITIONS - 1
-GPSIMD_FROM = 6
 FLOPS = 2 * BATCH * PAIRS * (2 * D * HIDDEN + HIDDEN * D)
 
 
@@ -144,10 +143,10 @@ def tile_lpair_kernel(tc, x, W1_words, W1_scales, b1, W2_words, W2_scales, b2, o
             first_half[sg] = a_b1
             norm2[sg] = grp.tile([P, columns_of[sg]], F32, tag="norm2", name="norm2")
 
-        def first_matmul(k):
-            sg, c, jb = tiles[k]
+        x_j_half = keep.tile([P, POSITIONS, HALVES, PACK, P], F32)
+
+        def second_half(jb):
             lhsT, lhsT_scale = x_slice(jb)
-            h_pre = work.tile([P, HALVES, PACK, P], F32, tag="h_pre")
             for h in range(HALVES):
                 cols = slice(D * h, D * (h + 1))
                 acc = ps_first.tile([P, D], F32, tag="first")
@@ -156,20 +155,25 @@ def tile_lpair_kernel(tc, x, W1_words, W1_scales, b1, W2_words, W2_scales, b2, o
                     rhs=w1_words[:, 1, cols].bitcast(FP8X4), rhs_scale=w1_scales[:, 1, cols],
                     start=True, stop=True,
                 )
-                nc.vector.tensor_tensor(
-                    out=h_pre[:, h, :, :],
-                    in0=acc[:].rearrange("r (p t) -> r t p", t=PACK),
-                    in1=first_half[sg][:, h, :, :],
-                    op=ALU.add,
-                )
-            pre[k] = h_pre
+                if h == 0:
+                    nc.vector.tensor_copy(out=x_j_half[:, jb, h, :, :], in_=acc[:].rearrange("r (p t) -> r t p", t=PACK))
+                else:
+                    nc.scalar.copy(out=x_j_half[:, jb, h, :, :], in_=acc[:].rearrange("r (p t) -> r t p", t=PACK))
 
         def turn_and_gelu(k):
+            sg, c, jb = tiles[k]
             h_grouped = work.tile([P, HALVES, P, PACK], BF16, tag="h_grouped", align_bytes=64)
             for h in range(HALVES):
                 turned = ps_turn.tile([P, PACK, P], F32, tag="turned")
                 for t in range(PACK):
-                    nc.tensor.transpose(turned[:, t, :], pre[k][:, h, t, :], ident[:])
+                    nc.tensor.matmul(
+                        out=turned[:, t, :], lhsT=first_half[sg][:, h, t, :], rhs=ident[:],
+                        is_transpose=True, start=True, stop=False,
+                    )
+                    nc.tensor.matmul(
+                        out=turned[:, t, :], lhsT=x_j_half[:, jb, h, t, :], rhs=ident[:],
+                        is_transpose=True, start=False, stop=True,
+                    )
                 nc.scalar.activation(
                     out=h_grouped[:, h, :, :],
                     in_=turned[:].rearrange("p t r -> p r t"),
@@ -255,21 +259,12 @@ def tile_lpair_kernel(tc, x, W1_words, W1_scales, b1, W2_words, W2_scales, b2, o
             n = columns_of[sg]
             weight = weight_of[sg]
             pooled = grp.tile([P, D], F32, tag="pooled")
-            if n >= GPSIMD_FROM:
-                nc.gpsimd.tensor_scalar(pooled[:], p_all[:, k_first, :], weight[:, 0:1], 0.0, ALU.mult, ALU.add)
-                for c in range(1, n):
-                    term = work.tile([P, D], F32, tag="term")
-                    nc.gpsimd.tensor_scalar(
-                        term[:], p_all[:, k_first + c, :], weight[:, c : c + 1], 0.0, ALU.mult, ALU.add
-                    )
-                    nc.gpsimd.tensor_tensor(out=pooled[:], in0=pooled[:], in1=term[:], op=ALU.add)
-            else:
-                nc.vector.tensor_scalar(pooled[:], p_all[:, k_first, :], weight[:, 0:1], None, ALU.mult)
-                for c in range(1, n):
-                    nc.vector.scalar_tensor_tensor(
-                        out=pooled[:], in0=p_all[:, k_first + c, :], scalar=weight[:, c : c + 1], in1=pooled[:],
-                        op0=ALU.mult, op1=ALU.add,
-                    )
+            nc.vector.tensor_scalar(pooled[:], p_all[:, k_first, :], weight[:, 0:1], None, ALU.mult)
+            for c in range(1, n):
+                nc.vector.scalar_tensor_tensor(
+                    out=pooled[:], in0=p_all[:, k_first + c, :], scalar=weight[:, c : c + 1], in1=pooled[:],
+                    op0=ALU.mult, op1=ALU.add,
+                )
             for s in range(2):
                 nc.sync.dma_start(out=out[:, 2 * sg + s, :], in_=pooled[BATCH * s : BATCH * (s + 1), :])
 
@@ -296,8 +291,8 @@ def tile_lpair_kernel(tc, x, W1_words, W1_scales, b1, W2_words, W2_scales, b2, o
                 if step == squares_done[sg] + 2:
                     weights(sg)
                     pool_and_store(sg, first_tile[sg])
-            if step < n_tiles:
-                first_matmul(step)
+            if step < columns_of[tiles[0][0]]:
+                second_half(tiles[step][2])
             if step + 1 < n_tiles and tiles[step + 1][1] == 0:
                 prepare_group(tiles[step + 1][0])
             if 0 <= step - 1 < n_tiles:

@@ -40,11 +40,15 @@ def tile_lpair_kernel(tc, x, W1_words, W1_scales, b1, W2_words, W2_scales, b2, o
         w1_scales = keep.tile([P, 2, HIDDEN], U8, align_bytes=64)
         w2_words = keep.tile([P, 2, D], U32, align_bytes=64)
         w2_scales = keep.tile([P, 2, D], U8, align_bytes=64)
-        b1_all = keep.tile([P, HIDDEN], BF16)
-        b2_all = keep.tile([P, D], BF16)
+        bias_rows = keep.tile([P, HIDDEN + D], BF16)
+        ones = keep.tile([P, P], BF16)
 
         nc.vector.memset(w1_scales[:].bitcast(I32), 0)
         nc.vector.memset(w2_scales[:].bitcast(I32), 0)
+        nc.vector.memset(bias_rows[:], 0.0)
+        nc.vector.memset(ones[:], 1.0)
+        nc.scalar.dma_start(out=bias_rows[0:1, 0:HIDDEN], in_=b1.unsqueeze(0))
+        nc.scalar.dma_start(out=bias_rows[0:1, HIDDEN:], in_=b2.unsqueeze(0))
 
         nc.sync.dma_start(out=x_sb[:], in_=x.rearrange("(a c) i d -> (c i) a d", a=4))
         for q in range(4):
@@ -67,13 +71,21 @@ def tile_lpair_kernel(tc, x, W1_words, W1_scales, b1, W2_words, W2_scales, b2, o
                 out=w2_words[:, g, :].bitcast(I32),
                 in_=W2_words[g].rearrange("p n t -> p (n t)").bitcast(I32),
             )
-        nc.scalar.dma_start(out=b1_all[:], in_=b1.partition_broadcast(P))
-        nc.scalar.dma_start(out=b2_all[:], in_=b2.partition_broadcast(P))
 
         ident = keep.tile([P, P], F32)
         make_identity(nc, ident[:])
         half = keep.tile([P, POSITIONS + 1], F32)
         nc.vector.memset(half[:], 0.5)
+
+        b1_sorted = keep.tile([P, HALVES, PACK, P], F32)
+        b2_all = keep.tile([P, D], F32)
+        for h in range(HALVES + 1):
+            spread = ps_first.tile([P, D], F32, tag="first")
+            nc.tensor.matmul(out=spread[:], lhsT=ones[:], rhs=bias_rows[:, D * h : D * (h + 1)], start=True, stop=True)
+            if h < HALVES:
+                nc.scalar.copy(out=b1_sorted[:, h, :, :], in_=spread[:].rearrange("r (p t) -> r t p", t=PACK))
+            else:
+                nc.scalar.copy(out=b2_all[:], in_=spread[:])
 
         x_grouped = keep.tile([P, POSITIONS, BATCH, PACK], BF16, align_bytes=64)
         x_grouped_words = x_grouped[:].rearrange("p i b t -> p i (b t)").bitcast(F32).rearrange(
@@ -123,6 +135,15 @@ def tile_lpair_kernel(tc, x, W1_words, W1_scales, b1, W2_words, W2_scales, b2, o
             cols = slice(BATCH * block, BATCH * block + P)
             return xq_words[:, cols].bitcast(FP8X4), xq_scales[:, cols]
 
+        def join(acc, addend, joined, h):
+            sorted_acc = acc[:].rearrange("r (p t) -> r t p", t=PACK)
+            if h == 0:
+                nc.vector.tensor_tensor(out=joined, in0=sorted_acc, in1=addend, op=ALU.add)
+            else:
+                raw = work.tile([P, PACK, P], F32, tag="raw")
+                nc.scalar.copy(out=raw[:], in_=sorted_acc)
+                nc.gpsimd.tensor_tensor(out=joined, in0=raw[:], in1=addend, op=ALU.add)
+
         def prepare_group(sg):
             lhsT, lhsT_scale = x_slice(2 * sg)
             a_b1 = grp.tile([P, HALVES, PACK, P], F32, tag="a_b1")
@@ -134,19 +155,14 @@ def tile_lpair_kernel(tc, x, W1_words, W1_scales, b1, W2_words, W2_scales, b2, o
                     rhs=w1_words[:, 0, cols].bitcast(FP8X4), rhs_scale=w1_scales[:, 0, cols],
                     start=True, stop=True,
                 )
-                nc.vector.tensor_tensor(
-                    out=a_b1[:, h, :, :],
-                    in0=acc[:].rearrange("r (p t) -> r t p", t=PACK),
-                    in1=b1_all[:, cols].rearrange("r (p t) -> r t p", t=PACK),
-                    op=ALU.add,
-                )
+                join(acc, b1_sorted[:, h, :, :], a_b1[:, h, :, :], h)
             first_half[sg] = a_b1
             norm2[sg] = grp.tile([P, columns_of[sg]], F32, tag="norm2", name="norm2")
 
-        x_j_half = keep.tile([P, POSITIONS, HALVES, PACK, P], F32)
-
-        def second_half(jb):
+        def first_matmul(k):
+            sg, c, jb = tiles[k]
             lhsT, lhsT_scale = x_slice(jb)
+            h_pre = work.tile([P, HALVES, PACK, P], F32, tag="h_pre")
             for h in range(HALVES):
                 cols = slice(D * h, D * (h + 1))
                 acc = ps_first.tile([P, D], F32, tag="first")
@@ -155,25 +171,15 @@ def tile_lpair_kernel(tc, x, W1_words, W1_scales, b1, W2_words, W2_scales, b2, o
                     rhs=w1_words[:, 1, cols].bitcast(FP8X4), rhs_scale=w1_scales[:, 1, cols],
                     start=True, stop=True,
                 )
-                if h == 0:
-                    nc.vector.tensor_copy(out=x_j_half[:, jb, h, :, :], in_=acc[:].rearrange("r (p t) -> r t p", t=PACK))
-                else:
-                    nc.scalar.copy(out=x_j_half[:, jb, h, :, :], in_=acc[:].rearrange("r (p t) -> r t p", t=PACK))
+                join(acc, first_half[sg][:, h, :, :], h_pre[:, h, :, :], h)
+            pre[k] = h_pre
 
         def turn_and_gelu(k):
-            sg, c, jb = tiles[k]
             h_grouped = work.tile([P, HALVES, P, PACK], BF16, tag="h_grouped", align_bytes=64)
             for h in range(HALVES):
                 turned = ps_turn.tile([P, PACK, P], F32, tag="turned")
                 for t in range(PACK):
-                    nc.tensor.matmul(
-                        out=turned[:, t, :], lhsT=first_half[sg][:, h, t, :], rhs=ident[:],
-                        is_transpose=True, start=True, stop=False,
-                    )
-                    nc.tensor.matmul(
-                        out=turned[:, t, :], lhsT=x_j_half[:, jb, h, t, :], rhs=ident[:],
-                        is_transpose=True, start=False, stop=True,
-                    )
+                    nc.tensor.transpose(turned[:, t, :], pre[k][:, h, t, :], ident[:])
                 nc.scalar.activation(
                     out=h_grouped[:, h, :, :],
                     in_=turned[:].rearrange("p t r -> p r t"),
@@ -291,8 +297,8 @@ def tile_lpair_kernel(tc, x, W1_words, W1_scales, b1, W2_words, W2_scales, b2, o
                 if step == squares_done[sg] + 2:
                     weights(sg)
                     pool_and_store(sg, first_tile[sg])
-            if step < columns_of[tiles[0][0]]:
-                second_half(tiles[step][2])
+            if step < n_tiles:
+                first_matmul(step)
             if step + 1 < n_tiles and tiles[step + 1][1] == 0:
                 prepare_group(tiles[step + 1][0])
             if 0 <= step - 1 < n_tiles:

@@ -22,6 +22,7 @@ HALVES = HIDDEN // D
 PACK = 4
 PAIRS = POSITIONS * (POSITIONS + 1) // 2
 WRAP_BLOCK = POSITIONS - 1
+POOLED_PER_STEP = 2
 FLOPS = 2 * BATCH * PAIRS * (2 * D * HIDDEN + HIDDEN * D)
 
 
@@ -29,11 +30,12 @@ def tile_lpair_kernel(tc, x, W1_words, W1_scales, b1, W2_words, W2_scales, b2, o
     nc = tc.nc
     with ExitStack() as ctx:
         keep = ctx.enter_context(tc.tile_pool(name="keep", bufs=1))
-        grp = ctx.enter_context(tc.tile_pool(name="grp", bufs=2))
+        grp = ctx.enter_context(tc.tile_pool(name="grp", bufs=4))
         work = ctx.enter_context(tc.tile_pool(name="work", bufs=3))
         ps_first = ctx.enter_context(tc.psum_pool(name="ps_first", bufs=3))
         ps_turn = ctx.enter_context(tc.psum_pool(name="ps_turn", bufs=3))
         ps_second = ctx.enter_context(tc.psum_pool(name="ps_second", bufs=2))
+        ctx.enter_context(tc.manual_schedule())
 
         x_sb = keep.tile([P, 4, D], BF16)
         w1_words = keep.tile([P, 2, HIDDEN], U32, align_bytes=64)
@@ -97,7 +99,8 @@ def tile_lpair_kernel(tc, x, W1_words, W1_scales, b1, W2_words, W2_scales, b2, o
             x_turned = ps_turn.tile([P, 2, P], F32, tag="turned")
             for u in range(2):
                 nc.tensor.transpose(x_turned[:, u, :], x_words[:, a, u : D // 2 : 2], ident[:])
-            nc.vector.tensor_copy(
+            copy_out = nc.vector.tensor_copy if a % 2 == 0 else nc.scalar.copy
+            copy_out(
                 out=x_grouped_words[:, :, rows_b * a : rows_b * (a + 1), :],
                 in_=x_turned[:].rearrange("p u (c i) -> p i c u", i=POSITIONS),
             )
@@ -219,7 +222,9 @@ def tile_lpair_kernel(tc, x, W1_words, W1_scales, b1, W2_words, W2_scales, b2, o
             )
 
         norm_of = {}
+        shift_of = {}
         tanh_of = {}
+        pooled_of = {}
         weight_of = {}
 
         def norms(sg):
@@ -228,7 +233,7 @@ def tile_lpair_kernel(tc, x, W1_words, W1_scales, b1, W2_words, W2_scales, b2, o
             nc.gpsimd.tensor_tensor(out=norm[:], in0=norm2[sg][:], in1=half[:, 0:n], op=ALU.pow)
             norm_of[sg] = norm
 
-        def shifted_tanh(sg):
+        def largest(sg):
             n = columns_of[sg]
             wrap = n - 1
             norm = norm_of[sg]
@@ -237,8 +242,11 @@ def tile_lpair_kernel(tc, x, W1_words, W1_scales, b1, W2_words, W2_scales, b2, o
             nc.vector.reduce_max(out=top[:], in_=norm[:], axis=AX.X)
             shift = grp.tile([P, 1], F32, tag="shift")
             nc.vector.tensor_scalar(shift[:], top[:], -0.5, None, ALU.mult)
-            th = grp.tile([P, n], F32, tag="th")
-            nc.scalar.activation(out=th[:], in_=norm[:], func=ACT.Tanh, bias=shift[:], scale=0.5)
+            shift_of[sg] = shift
+
+        def shifted_tanh(sg):
+            th = grp.tile([P, columns_of[sg]], F32, tag="th")
+            nc.scalar.activation(out=th[:], in_=norm_of[sg][:], func=ACT.Tanh, bias=shift_of[sg][:], scale=0.5)
             tanh_of[sg] = th
 
         def weights(sg):
@@ -261,18 +269,19 @@ def tile_lpair_kernel(tc, x, W1_words, W1_scales, b1, W2_words, W2_scales, b2, o
             nc.vector.tensor_scalar(weight[:], e[:], total[:], None, ALU.mult)
             weight_of[sg] = weight
 
-        def pool_and_store(sg, k_first):
-            n = columns_of[sg]
-            weight = weight_of[sg]
-            pooled = grp.tile([P, D], F32, tag="pooled")
-            nc.vector.tensor_scalar(pooled[:], p_all[:, k_first, :], weight[:, 0:1], None, ALU.mult)
-            for c in range(1, n):
+        def pool_tile(sg, c):
+            p_tile = p_all[:, first_tile[sg] + c, :]
+            w = weight_of[sg][:, c : c + 1]
+            if c == 0:
+                pooled_of[sg] = grp.tile([P, D], F32, tag="pooled", name="pooled")
+                nc.vector.tensor_scalar(pooled_of[sg][:], p_tile, w, None, ALU.mult)
+            else:
                 nc.vector.scalar_tensor_tensor(
-                    out=pooled[:], in0=p_all[:, k_first + c, :], scalar=weight[:, c : c + 1], in1=pooled[:],
-                    op0=ALU.mult, op1=ALU.add,
+                    out=pooled_of[sg][:], in0=p_tile, scalar=w, in1=pooled_of[sg][:], op0=ALU.mult, op1=ALU.add
                 )
-            for s in range(2):
-                nc.sync.dma_start(out=out[:, 2 * sg + s, :], in_=pooled[BATCH * s : BATCH * (s + 1), :])
+            if c == columns_of[sg] - 1:
+                for s in range(2):
+                    nc.sync.dma_start(out=out[:, 2 * sg + s, :], in_=pooled_of[sg][BATCH * s : BATCH * (s + 1), :])
 
         first_tile = {}
         squares_done = {}
@@ -282,21 +291,13 @@ def tile_lpair_kernel(tc, x, W1_words, W1_scales, b1, W2_words, W2_scales, b2, o
             squares_done[sg] = k + 4
 
         prepare_group(tiles[0][0])
-        for step in range(n_tiles + 7):
+        for step in range(n_tiles + 8):
             if 0 <= step - 2 < n_tiles:
                 quantise(step - 2)
             if 0 <= step - 3 < n_tiles:
                 add_b2(step - 3)
             if 0 <= step - 4 < n_tiles:
                 square(step - 4)
-            for sg in columns_of:
-                if step == squares_done[sg]:
-                    norms(sg)
-                if step == squares_done[sg] + 1:
-                    shifted_tanh(sg)
-                if step == squares_done[sg] + 2:
-                    weights(sg)
-                    pool_and_store(sg, first_tile[sg])
             if step < n_tiles:
                 first_matmul(step)
             if step + 1 < n_tiles and tiles[step + 1][1] == 0:
@@ -305,3 +306,14 @@ def tile_lpair_kernel(tc, x, W1_words, W1_scales, b1, W2_words, W2_scales, b2, o
                 turn_and_gelu(step - 1)
             if 0 <= step - 2 < n_tiles:
                 second_matmul(step - 2)
+            for sg in columns_of:
+                if step == squares_done[sg]:
+                    norms(sg)
+                if step == squares_done[sg] + 1:
+                    largest(sg)
+                    shifted_tanh(sg)
+                if step == squares_done[sg] + 2:
+                    weights(sg)
+                for c in range(columns_of[sg]):
+                    if step == squares_done[sg] + 3 + c // POOLED_PER_STEP:
+                        pool_tile(sg, c)

@@ -45,9 +45,9 @@ def tile_lpair_kernel(tc, x, W1_words, W1_scales, b1, W2_words, W2_scales, b2, o
         bias_rows = keep.tile([P, HIDDEN + D], BF16)
         ones = keep.tile([P, P], BF16)
 
+        nc.vector.memset(bias_rows[:], 0.0)
         nc.vector.memset(w1_scales[:].bitcast(I32), 0)
         nc.vector.memset(w2_scales[:].bitcast(I32), 0)
-        nc.vector.memset(bias_rows[:], 0.0)
         nc.vector.memset(ones[:], 1.0)
         nc.scalar.dma_start(out=bias_rows[0:1, 0:HIDDEN], in_=b1.unsqueeze(0))
         nc.scalar.dma_start(out=bias_rows[0:1, HIDDEN:], in_=b2.unsqueeze(0))
@@ -78,16 +78,8 @@ def tile_lpair_kernel(tc, x, W1_words, W1_scales, b1, W2_words, W2_scales, b2, o
         make_identity(nc, ident[:])
         half = keep.tile([P, POSITIONS + 1], F32)
         nc.vector.memset(half[:], 0.5)
-
-        b1_sorted = keep.tile([P, HALVES, PACK, P], F32)
-        b2_all = keep.tile([P, D], F32)
-        for h in range(HALVES + 1):
-            spread = ps_first.tile([P, D], F32, tag="first")
-            nc.tensor.matmul(out=spread[:], lhsT=ones[:], rhs=bias_rows[:, D * h : D * (h + 1)], start=True, stop=True)
-            if h < HALVES:
-                nc.scalar.copy(out=b1_sorted[:, h, :, :], in_=spread[:].rearrange("r (p t) -> r t p", t=PACK))
-            else:
-                nc.scalar.copy(out=b2_all[:], in_=spread[:])
+        one = keep.tile([P, POSITIONS + 1], F32)
+        nc.vector.memset(one[:], 1.0)
 
         x_grouped = keep.tile([P, POSITIONS, BATCH, PACK], BF16, align_bytes=64)
         x_grouped_words = x_grouped[:].rearrange("p i b t -> p i (b t)").bitcast(F32).rearrange(
@@ -104,6 +96,16 @@ def tile_lpair_kernel(tc, x, W1_words, W1_scales, b1, W2_words, W2_scales, b2, o
                 out=x_grouped_words[:, :, rows_b * a : rows_b * (a + 1), :],
                 in_=x_turned[:].rearrange("p u (c i) -> p i c u", i=POSITIONS),
             )
+        b1_sorted = keep.tile([P, HALVES, PACK, P], F32)
+        b2_all = keep.tile([P, D], F32)
+        for h in range(HALVES + 1):
+            spread = ps_first.tile([P, D], F32, tag="first")
+            nc.tensor.matmul(out=spread[:], lhsT=ones[:], rhs=bias_rows[:, D * h : D * (h + 1)], start=True, stop=True)
+            if h < HALVES:
+                nc.scalar.copy(out=b1_sorted[:, h, :, :], in_=spread[:].rearrange("r (p t) -> r t p", t=PACK))
+            else:
+                nc.scalar.copy(out=b2_all[:], in_=spread[:])
+
         xq_words = keep.tile([P, (POSITIONS + 1) * BATCH], U32, align_bytes=64)
         xq_scales = keep.tile([P, (POSITIONS + 1) * BATCH], U8, align_bytes=64)
         x_flat = x_grouped[:].rearrange("p i b t -> p (i b t)")
@@ -138,14 +140,11 @@ def tile_lpair_kernel(tc, x, W1_words, W1_scales, b1, W2_words, W2_scales, b2, o
             cols = slice(BATCH * block, BATCH * block + P)
             return xq_words[:, cols].bitcast(FP8X4), xq_scales[:, cols]
 
-        def join(acc, addend, joined, h):
-            sorted_acc = acc[:].rearrange("r (p t) -> r t p", t=PACK)
-            if h == 0:
-                nc.vector.tensor_tensor(out=joined, in0=sorted_acc, in1=addend, op=ALU.add)
-            else:
-                raw = work.tile([P, PACK, P], F32, tag="raw")
-                nc.scalar.copy(out=raw[:], in_=sorted_acc)
-                nc.gpsimd.tensor_tensor(out=joined, in0=raw[:], in1=addend, op=ALU.add)
+        def sorted_view(acc):
+            return acc[:].rearrange("r (p t) -> r t p", t=PACK)
+
+        x_j_kept = keep.tile([P, POSITIONS, PACK, P], F32)
+        kept = set()
 
         def prepare_group(sg):
             lhsT, lhsT_scale = x_slice(2 * sg)
@@ -158,7 +157,7 @@ def tile_lpair_kernel(tc, x, W1_words, W1_scales, b1, W2_words, W2_scales, b2, o
                     rhs=w1_words[:, 0, cols].bitcast(FP8X4), rhs_scale=w1_scales[:, 0, cols],
                     start=True, stop=True,
                 )
-                join(acc, b1_sorted[:, h, :, :], a_b1[:, h, :, :], h)
+                nc.vector.tensor_tensor(out=a_b1[:, h, :, :], in0=sorted_view(acc), in1=b1_sorted[:, h, :, :], op=ALU.add)
             first_half[sg] = a_b1
             norm2[sg] = grp.tile([P, columns_of[sg]], F32, tag="norm2", name="norm2")
 
@@ -167,6 +166,8 @@ def tile_lpair_kernel(tc, x, W1_words, W1_scales, b1, W2_words, W2_scales, b2, o
             lhsT, lhsT_scale = x_slice(jb)
             h_pre = work.tile([P, HALVES, PACK, P], F32, tag="h_pre")
             for h in range(HALVES):
+                if h == 1 and jb in kept:
+                    continue
                 cols = slice(D * h, D * (h + 1))
                 acc = ps_first.tile([P, D], F32, tag="first")
                 nc.tensor.matmul_mx(
@@ -174,7 +175,16 @@ def tile_lpair_kernel(tc, x, W1_words, W1_scales, b1, W2_words, W2_scales, b2, o
                     rhs=w1_words[:, 1, cols].bitcast(FP8X4), rhs_scale=w1_scales[:, 1, cols],
                     start=True, stop=True,
                 )
-                join(acc, first_half[sg][:, h, :, :], h_pre[:, h, :, :], h)
+                if h == 0:
+                    nc.vector.tensor_tensor(
+                        out=h_pre[:, 0, :, :], in0=sorted_view(acc), in1=first_half[sg][:, 0, :, :], op=ALU.add
+                    )
+                else:
+                    nc.scalar.copy(out=x_j_kept[:, jb, :, :], in_=sorted_view(acc))
+                    kept.add(jb)
+            nc.gpsimd.tensor_tensor(
+                out=h_pre[:, 1, :, :], in0=x_j_kept[:, jb, :, :], in1=first_half[sg][:, 1, :, :], op=ALU.add
+            )
             pre[k] = h_pre
 
         def turn_and_gelu(k):
@@ -218,7 +228,7 @@ def tile_lpair_kernel(tc, x, W1_words, W1_scales, b1, W2_words, W2_scales, b2, o
             sg, c, jb = tiles[k]
             squares = work.tile([P, D], BF16, tag="squares")
             nc.scalar.activation(
-                out=squares[:], in_=p_all[:, k, :], func=ACT.Square, accum_out=norm2[sg][:, c : c + 1]
+                out=squares[:], in_=p_all[:, k, :], func=ACT.Square, scale=0.5, accum_out=norm2[sg][:, c : c + 1]
             )
 
         norm_of = {}
@@ -237,32 +247,26 @@ def tile_lpair_kernel(tc, x, W1_words, W1_scales, b1, W2_words, W2_scales, b2, o
             n = columns_of[sg]
             wrap = n - 1
             norm = norm_of[sg]
-            nc.vector.tensor_copy(out=norm[0:BATCH, wrap : wrap + 1], in_=norm[0:BATCH, 0:1])
-            top = grp.tile([P, 1], F32, tag="top")
-            nc.vector.reduce_max(out=top[:], in_=norm[:], axis=AX.X)
+            nc.vector.memset(norm[0:BATCH, wrap : wrap + 1], -1.0e30)
             shift = grp.tile([P, 1], F32, tag="shift")
-            nc.vector.tensor_scalar(shift[:], top[:], -0.5, None, ALU.mult)
+            nc.vector.reduce_max(out=shift[:], in_=norm[:], axis=AX.X, negate=True)
             shift_of[sg] = shift
 
         def shifted_tanh(sg):
             th = grp.tile([P, columns_of[sg]], F32, tag="th")
-            nc.scalar.activation(out=th[:], in_=norm_of[sg][:], func=ACT.Tanh, bias=shift_of[sg][:], scale=0.5)
+            nc.scalar.activation(out=th[:], in_=norm_of[sg][:], func=ACT.Tanh, bias=shift_of[sg][:])
             tanh_of[sg] = th
 
         def weights(sg):
             n = columns_of[sg]
-            wrap = n - 1
             th = tanh_of[sg]
-            num = grp.tile([P, n], F32, tag="num")
-            nc.vector.tensor_scalar(num[:], th[:], 1.0, None, ALU.add)
-            nc.vector.memset(num[0:BATCH, wrap : wrap + 1], 0.0)
             den = grp.tile([P, n], F32, tag="den")
             nc.vector.tensor_scalar(den[:], th[:], -1.0, 1.0, ALU.mult, ALU.add)
             nc.vector.reciprocal(den[:], den[:])
             e = grp.tile([P, n], F32, tag="e")
             total = grp.tile([P, 1], F32, tag="total")
             nc.vector.scalar_tensor_tensor(
-                out=e[:], in0=num[:], scalar=1.0, in1=den[:], op0=ALU.mult, op1=ALU.mult, accum_out=total[:]
+                out=e[:], in0=den[:], scalar=2.0, in1=one[:, 0:n], op0=ALU.mult, op1=ALU.subtract, accum_out=total[:]
             )
             nc.vector.reciprocal(total[:], total[:])
             weight = grp.tile([P, n], F32, tag="weight")

@@ -21,9 +21,11 @@ HIDDEN = 1024
 HALVES = HIDDEN // D
 PACK = 4
 PAIRS = POSITIONS * (POSITIONS + 1) // 2
-WRAP_BLOCK = POSITIONS - 1
-POOLED_PER_STEP = 2
 FLOPS = 2 * BATCH * PAIRS * (2 * D * HIDDEN + HIDDEN * D)
+
+X_BLOCKS = (1, 0, 0, 1, 2, 3, 4, 5, 6, 7, 0, 7, 1, 5, 1, 3)
+NATURAL = 2
+POOLED_PER_STEP = 3
 
 
 def tile_lpair_kernel(tc, x, W1_words, W1_scales, b1, W2_words, W2_scales, b2, out):
@@ -32,37 +34,47 @@ def tile_lpair_kernel(tc, x, W1_words, W1_scales, b1, W2_words, W2_scales, b2, o
         keep = ctx.enter_context(tc.tile_pool(name="keep", bufs=1))
         grp = ctx.enter_context(tc.tile_pool(name="grp", bufs=4))
         work = ctx.enter_context(tc.tile_pool(name="work", bufs=3))
-        ps_first = ctx.enter_context(tc.psum_pool(name="ps_first", bufs=3))
-        ps_turn = ctx.enter_context(tc.psum_pool(name="ps_turn", bufs=3))
+        codes = ctx.enter_context(tc.tile_pool(name="codes", bufs=5))
+        ps_first = ctx.enter_context(tc.psum_pool(name="ps_first", bufs=6))
         ps_second = ctx.enter_context(tc.psum_pool(name="ps_second", bufs=2))
         ctx.enter_context(tc.manual_schedule())
 
         x_sb = keep.tile([P, 4, D], BF16)
-        w1_words = keep.tile([P, 2, HIDDEN], U32, align_bytes=64)
-        w1_scales = keep.tile([P, 2, HIDDEN], U8, align_bytes=64)
+        w1_raw = keep.tile([P, 2, HIDDEN], U32, align_bytes=64)
+        w1_raw_scales = keep.tile([P, 2, HIDDEN], U8, align_bytes=64)
+        w1_words = keep.tile([P, 2, HALVES, PACK, P], U32, align_bytes=64)
+        w1_scales = keep.tile([P, HALVES, 2, PACK, P], U8, align_bytes=64)
         w2_words = keep.tile([P, 2, D], U32, align_bytes=64)
         w2_scales = keep.tile([P, 2, D], U8, align_bytes=64)
-        bias_rows = keep.tile([P, HIDDEN + D], BF16)
+        b2_row = keep.tile([P, D], BF16)
         ones = keep.tile([P, P], BF16)
-
-        nc.vector.memset(bias_rows[:], 0.0)
-        nc.vector.memset(w1_scales[:].bitcast(I32), 0)
-        nc.vector.memset(w2_scales[:].bitcast(I32), 0)
-        nc.vector.memset(ones[:], 1.0)
-        nc.scalar.dma_start(out=bias_rows[0:1, 0:HIDDEN], in_=b1.unsqueeze(0))
-        nc.scalar.dma_start(out=bias_rows[0:1, HIDDEN:], in_=b2.unsqueeze(0))
+        b1_bf = keep.tile([P, HALVES, PACK], BF16)
+        b1_col = keep.tile([P, HALVES * PACK], F32)
+        warm = keep.tile([P, 1], F32)
+        warm_out = keep.tile([P, 1], F32)
 
         nc.sync.dma_start(out=x_sb[:], in_=x.rearrange("(a c) i d -> (c i) a d", a=4))
+        with nc.allow_non_contiguous_dma(reason="b1 lands with channel 4 p + t on partition p: runs of four values"):
+            nc.scalar.dma_start(out=b1_bf[:], in_=b1.rearrange("(h p t) -> p h t", h=HALVES, t=PACK))
+        nc.vector.memset(w1_raw_scales[:].bitcast(I32), 0)
+        nc.vector.memset(w2_scales[:].bitcast(I32), 0)
+        nc.vector.memset(b2_row[:], 0.0)
+        nc.scalar.dma_start(out=b2_row[0:1, :], in_=b2.unsqueeze(0))
+        nc.gpsimd.memset(warm[:], 0.0)
+        nc.scalar.activation(out=warm_out[:], in_=warm[:], func=ACT.Gelu)
+        nc.vector.memset(ones[:], 1.0)
+
         for q in range(4):
             nc.sync.dma_start(
-                out=w1_scales[32 * q : 32 * q + 4, :, :].bitcast(I32),
+                out=w1_raw_scales[32 * q : 32 * q + 4, :, :].bitcast(I32),
                 in_=W1_scales[:, 4 * q : 4 * q + 4, :].rearrange("g r n -> r g n").bitcast(I32),
             )
-        for g in range(2):
-            nc.sync.dma_start(
-                out=w1_words[:, g, :].bitcast(I32),
-                in_=W1_words[g].rearrange("p n t -> p (n t)").bitcast(I32),
-            )
+        for h in range(HALVES):
+            for g in range(2):
+                nc.sync.dma_start(
+                    out=w1_raw[:, g, D * h : D * (h + 1)].bitcast(I32),
+                    in_=W1_words[g].rearrange("p n t -> p (n t)")[:, PACK * D * h : PACK * D * (h + 1)].bitcast(I32),
+                )
         for q in range(4):
             nc.sync.dma_start(
                 out=w2_scales[32 * q : 32 * q + 4, :, :].bitcast(I32),
@@ -80,6 +92,13 @@ def tile_lpair_kernel(tc, x, W1_words, W1_scales, b1, W2_words, W2_scales, b2, o
         nc.vector.memset(half[:], 0.5)
         one = keep.tile([P, POSITIONS + 1], F32)
         nc.vector.memset(one[:], 1.0)
+        nc.gpsimd.tensor_copy(out=b1_col[:], in_=b1_bf[:].rearrange("p h t -> p (h t)"))
+
+        def sort_w1_scales(h):
+            nc.vector.tensor_copy(
+                out=w1_scales[:, h, :, :, :],
+                in_=w1_raw_scales[:, :, D * h : D * (h + 1)].rearrange("p g (m t) -> p g t m", t=PACK),
+            )
 
         x_grouped = keep.tile([P, POSITIONS, BATCH, PACK], BF16, align_bytes=64)
         x_grouped_words = x_grouped[:].rearrange("p i b t -> p i (b t)").bitcast(F32).rearrange(
@@ -88,51 +107,62 @@ def tile_lpair_kernel(tc, x, W1_words, W1_scales, b1, W2_words, W2_scales, b2, o
         x_words = x_sb[:].bitcast(F32)
         rows_b = BATCH // 4
         for a in range(4):
-            x_turned = ps_turn.tile([P, 2, P], F32, tag="turned")
+            x_turned = ps_first.tile([P, 2, P], F32, tag="first")
             for u in range(2):
                 nc.tensor.transpose(x_turned[:, u, :], x_words[:, a, u : D // 2 : 2], ident[:])
-            copy_out = nc.vector.tensor_copy if a % 2 == 0 else nc.scalar.copy
-            copy_out(
+            nc.scalar.copy(
                 out=x_grouped_words[:, :, rows_b * a : rows_b * (a + 1), :],
                 in_=x_turned[:].rearrange("p u (c i) -> p i c u", i=POSITIONS),
             )
-        b1_sorted = keep.tile([P, HALVES, PACK, P], F32)
-        b2_all = keep.tile([P, D], F32)
-        for h in range(HALVES + 1):
-            spread = ps_first.tile([P, D], F32, tag="first")
-            nc.tensor.matmul(out=spread[:], lhsT=ones[:], rhs=bias_rows[:, D * h : D * (h + 1)], start=True, stop=True)
-            if h < HALVES:
-                nc.scalar.copy(out=b1_sorted[:, h, :, :], in_=spread[:].rearrange("r (p t) -> r t p", t=PACK))
-            else:
-                nc.scalar.copy(out=b2_all[:], in_=spread[:])
+        xq_words = keep.tile([P, len(X_BLOCKS) * BATCH], U32, align_bytes=64)
+        xq_scales = keep.tile([P, len(X_BLOCKS) * BATCH], U8, align_bytes=64)
 
-        xq_words = keep.tile([P, (POSITIONS + 1) * BATCH], U32, align_bytes=64)
-        xq_scales = keep.tile([P, (POSITIONS + 1) * BATCH], U8, align_bytes=64)
-        x_flat = x_grouped[:].rearrange("p i b t -> p (i b t)")
-        nc.vector.quantize_mx(
-            out=xq_words[:, 0 : POSITIONS * BATCH].bitcast(FP8X4),
-            scales=xq_scales[:, 0 : POSITIONS * BATCH],
-            in_=x_flat,
-        )
-        nc.vector.quantize_mx(
-            out=xq_words[:, POSITIONS * BATCH :].bitcast(FP8X4),
-            scales=xq_scales[:, POSITIONS * BATCH :],
-            in_=x_flat[:, 0 : BATCH * PACK],
-        )
+        def quantise_x(first_block, n_blocks, position):
+            cols = slice(BATCH * first_block, BATCH * (first_block + n_blocks))
+            nc.vector.quantize_mx(
+                out=xq_words[:, cols].bitcast(FP8X4),
+                scales=xq_scales[:, cols],
+                in_=x_grouped[:, position : position + n_blocks, :, :].rearrange("p i b t -> p (i b t)"),
+            )
+
+        def sort_w1(g, h):
+            nc.vector.tensor_copy(
+                out=w1_words[:, g, h, :, :].bitcast(I32),
+                in_=w1_raw[:, g, D * h : D * (h + 1)].bitcast(I32).rearrange("p (m t) -> p t m", t=PACK),
+            )
+
+        sort_w1_scales(0)
+        sort_w1(0, 0)
+        quantise_x(NATURAL, POSITIONS, 0)
+        sort_w1(1, 0)
+        sort_w1_scales(1)
+        sort_w1(0, 1)
+        sort_w1(1, 1)
+        for block, position in enumerate(X_BLOCKS):
+            if not NATURAL <= block < NATURAL + POSITIONS:
+                quantise_x(block, 1, position)
 
         tiles = []
-        columns_of = {}
-        for sg in (3, 2, 1, 0):
-            blocks = list(range(2 * sg + 1)) + [WRAP_BLOCK]
-            columns_of[sg] = len(blocks)
-            for c, jb in enumerate(blocks):
-                tiles.append((sg, c, jb))
+        tiles += [(NATURAL + 6, NATURAL + j) for j in range(7)]
+        tiles += [(10, 1)]
+        tiles += [(NATURAL + 4, NATURAL + j) for j in range(5)]
+        tiles += [(12, 1)]
+        tiles += [(14, 0)]
+        tiles += [(NATURAL + 2, NATURAL + j) for j in range(3)]
         n_tiles = len(tiles)
+        units = [list(range(c, min(c + 4, n_tiles))) for c in range(0, n_tiles, 4)]
+        sums = [
+            (0, 8, 7, ((0, 6), (1, 7))),
+            (8, 14, 13, ((0, 4), (1, 5))),
+            (13, 15, None, ((0, 1),)),
+            (14, 18, 14, ((0, 2), (1, 3))),
+        ]
 
         p_all = keep.tile([P, n_tiles, D], F32)
-        first_half = {}
-        norm2 = {}
-        pre = {}
+        norm2 = keep.tile([P, n_tiles], F32)
+        b2_all = keep.tile([P, D], F32)
+        gelu_of = {}
+        grouped_of = {}
         hq = {}
         second = {}
 
@@ -140,95 +170,64 @@ def tile_lpair_kernel(tc, x, W1_words, W1_scales, b1, W2_words, W2_scales, b2, o
             cols = slice(BATCH * block, BATCH * block + P)
             return xq_words[:, cols].bitcast(FP8X4), xq_scales[:, cols]
 
-        def sorted_view(acc):
-            return acc[:].rearrange("r (p t) -> r t p", t=PACK)
-
-        x_j_kept = keep.tile([P, POSITIONS, PACK, P], F32)
-        kept = set()
-
-        def prepare_group(sg):
-            lhsT, lhsT_scale = x_slice(2 * sg)
-            a_b1 = grp.tile([P, HALVES, PACK, P], F32, tag="a_b1")
-            for h in range(HALVES):
-                cols = slice(D * h, D * (h + 1))
-                acc = ps_first.tile([P, D], F32, tag="first")
-                nc.tensor.matmul_mx(
-                    out=acc[:], lhsT=lhsT, lhsT_scale=lhsT_scale,
-                    rhs=w1_words[:, 0, cols].bitcast(FP8X4), rhs_scale=w1_scales[:, 0, cols],
-                    start=True, stop=True,
-                )
-                nc.vector.tensor_tensor(out=a_b1[:, h, :, :], in0=sorted_view(acc), in1=b1_sorted[:, h, :, :], op=ALU.add)
-            first_half[sg] = a_b1
-            norm2[sg] = grp.tile([P, columns_of[sg]], F32, tag="norm2", name="norm2")
-
-        def first_matmul(k):
-            sg, c, jb = tiles[k]
-            lhsT, lhsT_scale = x_slice(jb)
-            h_pre = work.tile([P, HALVES, PACK, P], F32, tag="h_pre")
-            for h in range(HALVES):
-                if h == 1 and jb in kept:
-                    continue
-                cols = slice(D * h, D * (h + 1))
-                acc = ps_first.tile([P, D], F32, tag="first")
-                nc.tensor.matmul_mx(
-                    out=acc[:], lhsT=lhsT, lhsT_scale=lhsT_scale,
-                    rhs=w1_words[:, 1, cols].bitcast(FP8X4), rhs_scale=w1_scales[:, 1, cols],
-                    start=True, stop=True,
-                )
-                if h == 0:
-                    nc.vector.tensor_tensor(
-                        out=h_pre[:, 0, :, :], in0=sorted_view(acc), in1=first_half[sg][:, 0, :, :], op=ALU.add
+        def first_bank(k, t):
+            s, h = divmod(k, 2)
+            rows = P * len(units[s])
+            if t == 0:
+                gelu_of[k] = work.tile([P, PACK, PACK * P], BF16, tag="gelu", name="gelu")
+            bank = ps_first.tile([P, PACK * P], F32, tag="first")
+            for q, c in enumerate(units[s]):
+                for g in range(2):
+                    rhs, rhs_scale = x_slice(tiles[c][g])
+                    nc.tensor.matmul_mx(
+                        out=bank[:, P * q : P * (q + 1)],
+                        lhsT=w1_words[:, g, h, t, :].bitcast(FP8X4), lhsT_scale=w1_scales[:, h, g, t, :],
+                        rhs=rhs, rhs_scale=rhs_scale,
+                        start=(g == 0), stop=(g == 1),
                     )
-                else:
-                    nc.scalar.copy(out=x_j_kept[:, jb, :, :], in_=sorted_view(acc))
-                    kept.add(jb)
-            nc.gpsimd.tensor_tensor(
-                out=h_pre[:, 1, :, :], in0=x_j_kept[:, jb, :, :], in1=first_half[sg][:, 1, :, :], op=ALU.add
+            nc.scalar.activation(
+                out=gelu_of[k][:, t, 0:rows], in_=bank[:, 0:rows], func=ACT.Gelu,
+                bias=b1_col[:, PACK * h + t : PACK * h + t + 1],
             )
-            pre[k] = h_pre
 
-        def turn_and_gelu(k):
-            h_grouped = work.tile([P, HALVES, P, PACK], BF16, tag="h_grouped", align_bytes=64)
-            for h in range(HALVES):
-                turned = ps_turn.tile([P, PACK, P], F32, tag="turned")
-                for t in range(PACK):
-                    nc.tensor.transpose(turned[:, t, :], pre[k][:, h, t, :], ident[:])
-                nc.scalar.activation(
-                    out=h_grouped[:, h, :, :],
-                    in_=turned[:].rearrange("p t r -> p r t"),
-                    func=ACT.Gelu,
-                )
-            pre[k] = h_grouped
+        def interleave(k):
+            rows = P * len(units[k // 2])
+            grouped = work.tile([P, PACK * P, PACK], BF16, tag="grouped", align_bytes=64)
+            nc.vector.tensor_copy(out=grouped[:, 0:rows, :], in_=gelu_of[k][:, :, 0:rows].rearrange("p t r -> p r t"))
+            grouped_of[k] = grouped
 
         def quantise(k):
-            words = work.tile([P, HALVES * P], U32, tag="hq_words", align_bytes=64)
-            scales = work.tile([P, HALVES * P], U8, tag="hq_scales", align_bytes=64)
+            rows = P * len(units[k // 2])
+            words = codes.tile([P, PACK * P], U32, tag="hq_words", align_bytes=64)
+            scales = codes.tile([P, PACK * P], U8, tag="hq_scales", align_bytes=64)
             nc.vector.quantize_mx(
-                out=words[:].bitcast(FP8X4), scales=scales[:],
-                in_=pre[k][:].rearrange("p h r t -> p (h r t)"),
+                out=words[:, 0:rows].bitcast(FP8X4), scales=scales[:, 0:rows],
+                in_=grouped_of[k][:, 0:rows, :].rearrange("p r t -> p (r t)"),
             )
             hq[k] = (words, scales)
 
-        def second_matmul(k):
-            words, scales = hq[k]
+        def second_matmul(c):
+            s, q = divmod(c, 4)
             acc = ps_second.tile([P, D], F32, tag="second")
             for h in range(HALVES):
-                rows = slice(P * h, P * (h + 1))
+                words, scales = hq[2 * s + h]
+                rows = slice(P * q, P * (q + 1))
                 nc.tensor.matmul_mx(
                     out=acc[:], lhsT=words[:, rows].bitcast(FP8X4), lhsT_scale=scales[:, rows],
                     rhs=w2_words[:, h, :].bitcast(FP8X4), rhs_scale=w2_scales[:, h, :],
                     start=(h == 0), stop=(h == HALVES - 1),
                 )
-            second[k] = acc
+            second[c] = acc
 
-        def add_b2(k):
-            nc.vector.tensor_tensor(out=p_all[:, k, :], in0=second[k][:], in1=b2_all[:], op=ALU.add)
+        def add_b2(c):
+            nc.vector.tensor_tensor(out=p_all[:, c, :], in0=second[c][:], in1=b2_all[:], op=ALU.add)
+            if c == 7:
+                nc.sync.dma_start(out=out[:, 0, :], in_=p_all[0:BATCH, c, :])
 
-        def square(k):
-            sg, c, jb = tiles[k]
+        def square(c):
             squares = work.tile([P, D], BF16, tag="squares")
             nc.scalar.activation(
-                out=squares[:], in_=p_all[:, k, :], func=ACT.Square, scale=0.5, accum_out=norm2[sg][:, c : c + 1]
+                out=squares[:], in_=p_all[:, c, :], func=ACT.Square, scale=0.5, accum_out=norm2[:, c : c + 1]
             )
 
         norm_of = {}
@@ -237,87 +236,116 @@ def tile_lpair_kernel(tc, x, W1_words, W1_scales, b1, W2_words, W2_scales, b2, o
         pooled_of = {}
         weight_of = {}
 
-        def norms(sg):
-            n = columns_of[sg]
-            norm = grp.tile([P, n], F32, tag="norm")
-            nc.gpsimd.tensor_tensor(out=norm[:], in0=norm2[sg][:], in1=half[:, 0:n], op=ALU.pow)
-            norm_of[sg] = norm
+        def norms(e):
+            c0, c1, masked, stored = sums[e]
+            norm = grp.tile([P, c1 - c0], F32, tag="norm")
+            nc.gpsimd.tensor_tensor(out=norm[:], in0=norm2[:, c0:c1], in1=half[:, 0 : c1 - c0], op=ALU.pow)
+            norm_of[e] = norm
 
-        def largest(sg):
-            n = columns_of[sg]
-            wrap = n - 1
-            norm = norm_of[sg]
-            nc.vector.memset(norm[0:BATCH, wrap : wrap + 1], -1.0e30)
+        def largest(e):
+            c0, c1, masked, stored = sums[e]
+            norm = norm_of[e]
+            if masked is not None:
+                nc.vector.memset(norm[0:BATCH, masked - c0 : masked - c0 + 1], -1.0e30)
             shift = grp.tile([P, 1], F32, tag="shift")
             nc.vector.reduce_max(out=shift[:], in_=norm[:], axis=AX.X, negate=True)
-            shift_of[sg] = shift
+            shift_of[e] = shift
 
-        def shifted_tanh(sg):
-            th = grp.tile([P, columns_of[sg]], F32, tag="th")
-            nc.scalar.activation(out=th[:], in_=norm_of[sg][:], func=ACT.Tanh, bias=shift_of[sg][:])
-            tanh_of[sg] = th
+        def shifted_tanh(e):
+            c0, c1, masked, stored = sums[e]
+            th = grp.tile([P, c1 - c0], F32, tag="th")
+            nc.scalar.activation(out=th[:], in_=norm_of[e][:], func=ACT.Tanh, bias=shift_of[e][:])
+            tanh_of[e] = th
 
-        def weights(sg):
-            n = columns_of[sg]
-            th = tanh_of[sg]
+        def weights(e):
+            c0, c1, masked, stored = sums[e]
+            n = c1 - c0
+            th = tanh_of[e]
             den = grp.tile([P, n], F32, tag="den")
             nc.vector.tensor_scalar(den[:], th[:], -1.0, 1.0, ALU.mult, ALU.add)
             nc.vector.reciprocal(den[:], den[:])
-            e = grp.tile([P, n], F32, tag="e")
+            ex = grp.tile([P, n], F32, tag="ex")
             total = grp.tile([P, 1], F32, tag="total")
             nc.vector.scalar_tensor_tensor(
-                out=e[:], in0=den[:], scalar=2.0, in1=one[:, 0:n], op0=ALU.mult, op1=ALU.subtract, accum_out=total[:]
+                out=ex[:], in0=den[:], scalar=2.0, in1=one[:, 0:n], op0=ALU.mult, op1=ALU.subtract, accum_out=total[:]
             )
             nc.vector.reciprocal(total[:], total[:])
             weight = grp.tile([P, n], F32, tag="weight")
-            nc.vector.tensor_scalar(weight[:], e[:], total[:], None, ALU.mult)
-            weight_of[sg] = weight
+            nc.vector.tensor_scalar(weight[:], ex[:], total[:], None, ALU.mult)
+            weight_of[e] = weight
 
-        def pool_tile(sg, c):
-            p_tile = p_all[:, first_tile[sg] + c, :]
-            w = weight_of[sg][:, c : c + 1]
-            if c == 0:
-                pooled_of[sg] = grp.tile([P, D], F32, tag="pooled", name="pooled")
-                nc.vector.tensor_scalar(pooled_of[sg][:], p_tile, w, None, ALU.mult)
+        def pool_tile(e, c):
+            c0, c1, masked, stored = sums[e]
+            w = weight_of[e][:, c - c0 : c - c0 + 1]
+            if c == c0:
+                pooled_of[e] = grp.tile([P, D], F32, tag="pooled", name="pooled")
+                nc.vector.tensor_scalar(pooled_of[e][:], p_all[:, c, :], w, None, ALU.mult)
             else:
                 nc.vector.scalar_tensor_tensor(
-                    out=pooled_of[sg][:], in0=p_tile, scalar=w, in1=pooled_of[sg][:], op0=ALU.mult, op1=ALU.add
+                    out=pooled_of[e][:], in0=p_all[:, c, :], scalar=w, in1=pooled_of[e][:], op0=ALU.mult, op1=ALU.add
                 )
-            if c == columns_of[sg] - 1:
-                for s in range(2):
-                    nc.sync.dma_start(out=out[:, 2 * sg + s, :], in_=pooled_of[sg][BATCH * s : BATCH * (s + 1), :])
+            if c == c1 - 1:
+                for s, i in stored:
+                    nc.sync.dma_start(out=out[:, i, :], in_=pooled_of[e][BATCH * s : BATCH * (s + 1), :])
 
-        first_tile = {}
-        squares_done = {}
-        for k, (sg, c, jb) in enumerate(tiles):
-            if c == 0:
-                first_tile[sg] = k
-            squares_done[sg] = k + 4
+        n_first = 2 * len(units)
+        second_at = {}
+        for s, unit in enumerate(units):
+            second_at.setdefault(2 * s + 3, []).extend(unit[0:2])
+            second_at.setdefault(2 * s + 4, []).extend(unit[2:4])
+        last_of = {sums[e][1] - 1: e for e in range(len(sums))}
 
-        prepare_group(tiles[0][0])
-        for step in range(n_tiles + 8):
-            if 0 <= step - 2 < n_tiles:
-                quantise(step - 2)
-            if 0 <= step - 3 < n_tiles:
-                add_b2(step - 3)
-            if 0 <= step - 4 < n_tiles:
-                square(step - 4)
-            if step < n_tiles:
-                first_matmul(step)
-            if step + 1 < n_tiles and tiles[step + 1][1] == 0:
-                prepare_group(tiles[step + 1][0])
-            if 0 <= step - 1 < n_tiles:
-                turn_and_gelu(step - 1)
-            if 0 <= step - 2 < n_tiles:
-                second_matmul(step - 2)
-            for sg in columns_of:
-                if step == squares_done[sg]:
-                    norms(sg)
-                if step == squares_done[sg] + 1:
-                    largest(sg)
-                    shifted_tanh(sg)
-                if step == squares_done[sg] + 2:
-                    weights(sg)
-                for c in range(columns_of[sg]):
-                    if step == squares_done[sg] + 3 + c // POOLED_PER_STEP:
-                        pool_tile(sg, c)
+        to_square = []
+        to_norm = []
+        to_max = []
+        to_weigh = []
+        waiting = []
+        step = 0
+        finished = 0
+        while finished < len(sums) or waiting:
+            running = step < n_first
+            arrived = second_at.get(step, [])
+            for c in arrived:
+                second_matmul(c)
+            for c in to_square:
+                square(c)
+                if c in last_of:
+                    to_norm.append(last_of[c])
+            to_square = []
+            for e in to_norm:
+                norms(e)
+                to_max.append(e)
+            to_norm = []
+            if 0 <= step - 1 < n_first:
+                interleave(step - 1)
+            for e in to_weigh:
+                weights(e)
+                waiting.extend([(e, c) for c in range(sums[e][0], sums[e][1])])
+                finished += 1
+            to_weigh = []
+            if arrived:
+                add_b2(arrived[0])
+            if 0 <= step - 1 < n_first:
+                quantise(step - 1)
+            for c in arrived[1:]:
+                add_b2(c)
+            to_square.extend(arrived)
+            for e in to_max:
+                largest(e)
+            for t in range(PACK):
+                if running:
+                    first_bank(step, t)
+                if t == 1:
+                    for e in to_max:
+                        shifted_tanh(e)
+                        to_weigh.append(e)
+                    to_max = []
+            if step == 0:
+                spread = ps_first.tile([P, D], F32, tag="first")
+                nc.tensor.matmul(out=spread[:], lhsT=ones[:], rhs=b2_row[:], start=True, stop=True)
+                nc.scalar.copy(out=b2_all[:], in_=spread[:])
+            quota = POOLED_PER_STEP
+            for e, c in waiting[0:quota]:
+                pool_tile(e, c)
+            waiting = waiting[quota:]
+            step += 1

@@ -23,7 +23,16 @@ PACK = 4
 PAIRS = POSITIONS * (POSITIONS + 1) // 2
 FLOPS = 2 * BATCH * PAIRS * (2 * D * HIDDEN + HIDDEN * D)
 
-X_BLOCKS = (1, 0, 0, 1, 2, 3, 4, 5, 6, 7, 0, 7, 1, 5, 1, 3)
+X_BLOCKS = (
+    1, 0, 0, 1, 2, 3, 4, 5, 6, 7,
+    6, 7, 6, 7, 0, 7,
+    4, 5, 4, 5, 1, 5,
+    1, 3, 2, 3, 2, 3,
+    5, 6, 0, 0,
+    4, 5, 0, 0,
+    2, 3, 1, 2,
+)
+RUNS = ((10, 2), (10, 6), (10, 3), (12, 28), (16, 2), (16, 3), (18, 32), (22, 0), (24, 36))
 NATURAL = 2
 POOLED_PER_STEP = 3
 
@@ -37,7 +46,6 @@ def tile_lpair_kernel(tc, x, W1_words, W1_scales, b1, W2_words, W2_scales, b2, o
         codes = ctx.enter_context(tc.tile_pool(name="codes", bufs=5))
         ps_first = ctx.enter_context(tc.psum_pool(name="ps_first", bufs=6))
         ps_second = ctx.enter_context(tc.psum_pool(name="ps_second", bufs=2))
-        ctx.enter_context(tc.manual_schedule())
 
         x_sb = keep.tile([P, 4, D], BF16)
         w1_raw = keep.tile([P, 2, HIDDEN], U32, align_bytes=64)
@@ -138,18 +146,21 @@ def tile_lpair_kernel(tc, x, W1_words, W1_scales, b1, W2_words, W2_scales, b2, o
         sort_w1_scales(1)
         sort_w1(0, 1)
         sort_w1(1, 1)
-        for block, position in enumerate(X_BLOCKS):
-            if not NATURAL <= block < NATURAL + POSITIONS:
-                quantise_x(block, 1, position)
+        made = set(range(NATURAL, NATURAL + POSITIONS))
+        for run in RUNS:
+            for first in run:
+                for block in range(first, first + 4, 2):
+                    if block in made:
+                        continue
+                    made.add(block)
+                    made.add(block + 1)
+                    if X_BLOCKS[block + 1] == X_BLOCKS[block] + 1:
+                        quantise_x(block, 2, X_BLOCKS[block])
+                    else:
+                        quantise_x(block, 1, X_BLOCKS[block])
+                        quantise_x(block + 1, 1, X_BLOCKS[block + 1])
 
-        tiles = []
-        tiles += [(NATURAL + 6, NATURAL + j) for j in range(7)]
-        tiles += [(10, 1)]
-        tiles += [(NATURAL + 4, NATURAL + j) for j in range(5)]
-        tiles += [(12, 1)]
-        tiles += [(14, 0)]
-        tiles += [(NATURAL + 2, NATURAL + j) for j in range(3)]
-        n_tiles = len(tiles)
+        n_tiles = 2 * len(RUNS)
         units = [list(range(c, min(c + 4, n_tiles))) for c in range(0, n_tiles, 4)]
         sums = [
             (0, 8, 7, ((0, 6), (1, 7))),
@@ -167,7 +178,7 @@ def tile_lpair_kernel(tc, x, W1_words, W1_scales, b1, W2_words, W2_scales, b2, o
         second = {}
 
         def x_slice(block):
-            cols = slice(BATCH * block, BATCH * block + P)
+            cols = slice(BATCH * block, BATCH * block + 2 * P)
             return xq_words[:, cols].bitcast(FP8X4), xq_scales[:, cols]
 
         def first_bank(k, t):
@@ -176,11 +187,11 @@ def tile_lpair_kernel(tc, x, W1_words, W1_scales, b1, W2_words, W2_scales, b2, o
             if t == 0:
                 gelu_of[k] = work.tile([P, PACK, PACK * P], BF16, tag="gelu", name="gelu")
             bank = ps_first.tile([P, PACK * P], F32, tag="first")
-            for q, c in enumerate(units[s]):
+            for q, c in enumerate(units[s][0::2]):
                 for g in range(2):
-                    rhs, rhs_scale = x_slice(tiles[c][g])
+                    rhs, rhs_scale = x_slice(RUNS[c // 2][g])
                     nc.tensor.matmul_mx(
-                        out=bank[:, P * q : P * (q + 1)],
+                        out=bank[:, 2 * P * q : 2 * P * (q + 1)],
                         lhsT=w1_words[:, g, h, t, :].bitcast(FP8X4), lhsT_scale=w1_scales[:, h, g, t, :],
                         rhs=rhs, rhs_scale=rhs_scale,
                         start=(g == 0), stop=(g == 1),

@@ -204,7 +204,10 @@ def tile_lpair_kernel(tc, x, W1_words, W1_scales, b1, W2_words, W2_scales, b2, o
         def interleave(k):
             rows = P * len(units[k // 2])
             grouped = work.tile([P, PACK * P, PACK], BF16, tag="grouped", align_bytes=64)
-            nc.vector.tensor_copy(out=grouped[:, 0:rows, :], in_=gelu_of[k][:, :, 0:rows].rearrange("p t r -> p r t"))
+            nc.vector.tensor_copy(
+                out=grouped[:, 0:rows, :].rearrange("p (c i) t -> p c t i", i=PACK),
+                in_=gelu_of[k][:, :, 0:rows].rearrange("p t (c i) -> p c t i", i=PACK),
+            )
             grouped_of[k] = grouped
 
         def quantise(k):

@@ -35,6 +35,7 @@ X_BLOCKS = (
 RUNS = ((10, 2), (10, 6), (10, 3), (12, 28), (16, 2), (16, 3), (18, 32), (22, 0), (24, 36))
 NATURAL = 2
 POOLED_PER_STEP = 3
+WARMING_MATMULS = 4
 
 
 def tile_lpair_kernel(tc, x, W1_words, W1_scales, b1, W2_words, W2_scales, b2, out):
@@ -49,13 +50,11 @@ def tile_lpair_kernel(tc, x, W1_words, W1_scales, b1, W2_words, W2_scales, b2, o
 
         x_sb = keep.tile([P, 4, D], BF16)
         w1_raw = keep.tile([P, 2, HIDDEN], U32, align_bytes=64)
-        w1_raw_scales = keep.tile([P, 2, HIDDEN], U8, align_bytes=64)
+        w1_raw_scales = keep.tile([P, HIDDEN], U8, align_bytes=64)
         w1_words = keep.tile([P, 2, HALVES, PACK, P], U32, align_bytes=64)
-        w1_scales = keep.tile([P, HALVES, 2, PACK, P], U8, align_bytes=64)
+        w1_scales = keep.tile([P, HALVES, PACK, P], U8, align_bytes=64)
         w2_words = keep.tile([P, 2, D], U32, align_bytes=64)
-        w2_scales = keep.tile([P, 2, D], U8, align_bytes=64)
-        b2_row = keep.tile([P, D], BF16)
-        ones = keep.tile([P, P], BF16)
+        w2_scales = keep.tile([P, D], U8, align_bytes=64)
         b1_bf = keep.tile([P, HALVES, PACK], BF16)
         b1_col = keep.tile([P, HALVES * PACK], F32)
         warm = keep.tile([P, 1], F32)
@@ -66,16 +65,13 @@ def tile_lpair_kernel(tc, x, W1_words, W1_scales, b1, W2_words, W2_scales, b2, o
             nc.scalar.dma_start(out=b1_bf[:], in_=b1.rearrange("(h p t) -> p h t", h=HALVES, t=PACK))
         nc.vector.memset(w1_raw_scales[:].bitcast(I32), 0)
         nc.vector.memset(w2_scales[:].bitcast(I32), 0)
-        nc.vector.memset(b2_row[:], 0.0)
-        nc.scalar.dma_start(out=b2_row[0:1, :], in_=b2.unsqueeze(0))
         nc.gpsimd.memset(warm[:], 0.0)
         nc.scalar.activation(out=warm_out[:], in_=warm[:], func=ACT.Gelu)
-        nc.vector.memset(ones[:], 1.0)
 
         for q in range(4):
             nc.sync.dma_start(
-                out=w1_raw_scales[32 * q : 32 * q + 4, :, :].bitcast(I32),
-                in_=W1_scales[:, 4 * q : 4 * q + 4, :].rearrange("g r n -> r g n").bitcast(I32),
+                out=w1_raw_scales[32 * q : 32 * q + 8, :].bitcast(I32),
+                in_=W1_scales[:, 4 * q : 4 * q + 4, :].bitcast(I32),
             )
         for h in range(HALVES):
             for g in range(2):
@@ -85,8 +81,8 @@ def tile_lpair_kernel(tc, x, W1_words, W1_scales, b1, W2_words, W2_scales, b2, o
                 )
         for q in range(4):
             nc.sync.dma_start(
-                out=w2_scales[32 * q : 32 * q + 4, :, :].bitcast(I32),
-                in_=W2_scales[:, 4 * q : 4 * q + 4, :].rearrange("g r n -> r g n").bitcast(I32),
+                out=w2_scales[32 * q : 32 * q + 8, :].bitcast(I32),
+                in_=W2_scales[:, 4 * q : 4 * q + 4, :].bitcast(I32),
             )
         for g in range(2):
             nc.sync.dma_start(
@@ -104,8 +100,8 @@ def tile_lpair_kernel(tc, x, W1_words, W1_scales, b1, W2_words, W2_scales, b2, o
 
         def sort_w1_scales(h):
             nc.vector.tensor_copy(
-                out=w1_scales[:, h, :, :, :],
-                in_=w1_raw_scales[:, :, D * h : D * (h + 1)].rearrange("p g (m t) -> p g t m", t=PACK),
+                out=w1_scales[:, h, :, :],
+                in_=w1_raw_scales[:, D * h : D * (h + 1)].rearrange("p (m t) -> p t m", t=PACK),
             )
 
         x_grouped = keep.tile([P, POSITIONS, BATCH, PACK], BF16, align_bytes=64)
@@ -122,6 +118,9 @@ def tile_lpair_kernel(tc, x, W1_words, W1_scales, b1, W2_words, W2_scales, b2, o
                 out=x_grouped_words[:, :, rows_b * a : rows_b * (a + 1), :],
                 in_=x_turned[:].rearrange("p u (c i) -> p i c u", i=POSITIONS),
             )
+        idle_bank = ps_first.tile([P, D], F32, tag="first")
+        for a in range(WARMING_MATMULS):
+            nc.tensor.matmul(out=idle_bank[:], lhsT=x_sb[:, a, 0:P], rhs=x_sb[:, a, :], start=True, stop=True)
         xq_words = keep.tile([P, len(X_BLOCKS) * BATCH], U32, align_bytes=64)
         xq_scales = keep.tile([P, len(X_BLOCKS) * BATCH], U8, align_bytes=64)
 
@@ -171,7 +170,8 @@ def tile_lpair_kernel(tc, x, W1_words, W1_scales, b1, W2_words, W2_scales, b2, o
 
         p_all = keep.tile([P, n_tiles, D], F32)
         norm2 = keep.tile([P, n_tiles], F32)
-        b2_all = keep.tile([P, D], F32)
+        b2_all = keep.tile([P, D], BF16)
+        nc.sync.dma_start(out=b2_all[:], in_=b2.partition_broadcast(P))
         gelu_of = {}
         grouped_of = {}
         hq = {}
@@ -192,7 +192,7 @@ def tile_lpair_kernel(tc, x, W1_words, W1_scales, b1, W2_words, W2_scales, b2, o
                     rhs, rhs_scale = x_slice(RUNS[c // 2][g])
                     nc.tensor.matmul_mx(
                         out=bank[:, 2 * P * q : 2 * P * (q + 1)],
-                        lhsT=w1_words[:, g, h, t, :].bitcast(FP8X4), lhsT_scale=w1_scales[:, h, g, t, :],
+                        lhsT=w1_words[:, g, h, t, :].bitcast(FP8X4), lhsT_scale=w1_scales[4 * g : P, h, t, :],
                         rhs=rhs, rhs_scale=rhs_scale,
                         start=(g == 0), stop=(g == 1),
                     )
@@ -228,7 +228,7 @@ def tile_lpair_kernel(tc, x, W1_words, W1_scales, b1, W2_words, W2_scales, b2, o
                 rows = slice(P * q, P * (q + 1))
                 nc.tensor.matmul_mx(
                     out=acc[:], lhsT=words[:, rows].bitcast(FP8X4), lhsT_scale=scales[:, rows],
-                    rhs=w2_words[:, h, :].bitcast(FP8X4), rhs_scale=w2_scales[:, h, :],
+                    rhs=w2_words[:, h, :].bitcast(FP8X4), rhs_scale=w2_scales[4 * h : P, :],
                     start=(h == 0), stop=(h == HALVES - 1),
                 )
             second[c] = acc
@@ -354,10 +354,6 @@ def tile_lpair_kernel(tc, x, W1_words, W1_scales, b1, W2_words, W2_scales, b2, o
                         shifted_tanh(e)
                         to_weigh.append(e)
                     to_max = []
-            if step == 0:
-                spread = ps_first.tile([P, D], F32, tag="first")
-                nc.tensor.matmul(out=spread[:], lhsT=ones[:], rhs=b2_row[:], start=True, stop=True)
-                nc.scalar.copy(out=b2_all[:], in_=spread[:])
             quota = POOLED_PER_STEP
             for e, c in waiting[0:quota]:
                 pool_tile(e, c)

@@ -25,14 +25,14 @@ FLOPS = 2 * BATCH * PAIRS * (2 * D * HIDDEN + HIDDEN * D)
 
 X_BLOCKS = (
     1, 0, 0, 1, 2, 3, 4, 5, 6, 7,
-    6, 7, 6, 7, 0, 7,
+    6, 7, 0, 7,
     4, 5, 4, 5, 1, 5,
     1, 3, 2, 3, 2, 3,
     5, 6, 0, 0,
     4, 5, 0, 0,
     2, 3, 1, 2,
 )
-RUNS = ((10, 2), (10, 6), (10, 3), (12, 28), (16, 2), (16, 3), (18, 32), (22, 0), (24, 36))
+RUNS = ((8, 2), (8, 6), (8, 3), (10, 26), (14, 2), (14, 3), (16, 30), (20, 0), (22, 34))
 NATURAL = 2
 POOLED_PER_STEP = 3
 WARMING_MATMULS = 4
@@ -138,26 +138,32 @@ def tile_lpair_kernel(tc, x, W1_words, W1_scales, b1, W2_words, W2_scales, b2, o
                 in_=w1_raw[:, g, D * h : D * (h + 1)].bitcast(I32).rearrange("p (m t) -> p t m", t=PACK),
             )
 
-        sort_w1_scales(0)
-        sort_w1(0, 0)
-        quantise_x(NATURAL, POSITIONS, 0)
-        sort_w1(1, 0)
-        sort_w1_scales(1)
-        sort_w1(0, 1)
-        sort_w1(1, 1)
         made = set(range(NATURAL, NATURAL + POSITIONS))
-        for run in RUNS:
-            for first in run:
-                for block in range(first, first + 4, 2):
-                    if block in made:
-                        continue
-                    made.add(block)
-                    made.add(block + 1)
-                    if X_BLOCKS[block + 1] == X_BLOCKS[block] + 1:
-                        quantise_x(block, 2, X_BLOCKS[block])
-                    else:
-                        quantise_x(block, 1, X_BLOCKS[block])
-                        quantise_x(block + 1, 1, X_BLOCKS[block + 1])
+
+        def quantise_blocks_of(runs):
+            for run in runs:
+                for first in run:
+                    for block in range(first, first + 4, 2):
+                        if block in made:
+                            continue
+                        made.add(block)
+                        made.add(block + 1)
+                        if X_BLOCKS[block + 1] == X_BLOCKS[block] + 1:
+                            quantise_x(block, 2, X_BLOCKS[block])
+                        else:
+                            quantise_x(block, 1, X_BLOCKS[block])
+                            quantise_x(block + 1, 1, X_BLOCKS[block + 1])
+
+        with tc.manual_schedule(engines={mybir.EngineType.DVE}):
+            sort_w1_scales(0)
+            sort_w1(0, 0)
+            sort_w1(1, 0)
+            quantise_x(NATURAL, POSITIONS, 0)
+            quantise_blocks_of(RUNS[0:2])
+            sort_w1_scales(1)
+            sort_w1(0, 1)
+            sort_w1(1, 1)
+            quantise_blocks_of(RUNS[2:])
 
         n_tiles = 2 * len(RUNS)
         units = [list(range(c, min(c + 4, n_tiles))) for c in range(0, n_tiles, 4)]

from contextlib import ExitStack

import concourse.mybir as mybir
from concourse.masks import make_identity

F32 = mybir.dt.float32
BF16 = mybir.dt.bfloat16
I32 = mybir.dt.int32
U32 = mybir.dt.uint32
U8 = mybir.dt.uint8
FP8X4 = mybir.dt.float8_e4m3fn_x4
ALU = mybir.AluOpType
ACT = mybir.ActivationFunctionType
AX = mybir.AxisListType

P = 128
BATCH = 64
POSITIONS = 8
D = 512
HIDDEN = 1024
HALVES = HIDDEN // D
PACK = 4
PAIRS = POSITIONS * (POSITIONS + 1) // 2
FLOPS = 2 * BATCH * PAIRS * (2 * D * HIDDEN + HIDDEN * D)

X_BLOCKS = (
    1, 0, 0, 1, 2, 3, 4, 5, 6, 7,
    6, 7, 0, 7,
    4, 5, 4, 5, 1, 5,
    1, 3, 2, 3, 2, 3,
    5, 6, 0, 0,
    4, 5, 0, 0,
    2, 3, 1, 2,
)
RUNS = ((8, 2), (8, 6), (8, 3), (10, 26), (14, 2), (14, 3), (16, 30), (20, 0), (22, 34))
NATURAL = 2
POOLED_PER_STEP = 3
WARMING_MATMULS = 4


def tile_lpair_kernel(tc, x, W1_words, W1_scales, b1, W2_words, W2_scales, b2, out):
    nc = tc.nc
    with ExitStack() as ctx:
        keep = ctx.enter_context(tc.tile_pool(name="keep", bufs=1))
        grp = ctx.enter_context(tc.tile_pool(name="grp", bufs=4))
        work = ctx.enter_context(tc.tile_pool(name="work", bufs=3))
        codes = ctx.enter_context(tc.tile_pool(name="codes", bufs=5))
        ps_first = ctx.enter_context(tc.psum_pool(name="ps_first", bufs=6))
        ps_second = ctx.enter_context(tc.psum_pool(name="ps_second", bufs=2))

        x_sb = keep.tile([P, 4, D], BF16)
        w1_raw = keep.tile([P, 2, HIDDEN], U32, align_bytes=64)
        w1_raw_scales = keep.tile([P, HIDDEN], U8, align_bytes=64)
        w1_words = keep.tile([P, 2, HALVES, PACK, P], U32, align_bytes=64)
        w1_scales = keep.tile([P, HALVES, PACK, P], U8, align_bytes=64)
        w2_words = keep.tile([P, 2, D], U32, align_bytes=64)
        w2_scales = keep.tile([P, D], U8, align_bytes=64)
        b1_bf = keep.tile([P, HALVES, PACK], BF16)
        b1_col = keep.tile([P, HALVES * PACK], F32)
        warm = keep.tile([P, 1], F32)
        warm_out = keep.tile([P, 1], F32)

        nc.sync.dma_start(out=x_sb[:], in_=x.rearrange("(a c) i d -> (c i) a d", a=4))
        with nc.allow_non_contiguous_dma(reason="b1 lands with channel 4 p + t on partition p: runs of four values"):
            nc.scalar.dma_start(out=b1_bf[:], in_=b1.rearrange("(h p t) -> p h t", h=HALVES, t=PACK))
        nc.vector.memset(w1_raw_scales[:].bitcast(I32), 0)
        nc.vector.memset(w2_scales[:].bitcast(I32), 0)
        nc.gpsimd.memset(warm[:], 0.0)
        nc.scalar.activation(out=warm_out[:], in_=warm[:], func=ACT.Gelu)

        for q in range(4):
            nc.sync.dma_start(
                out=w1_raw_scales[32 * q : 32 * q + 8, :].bitcast(I32),
                in_=W1_scales[:, 4 * q : 4 * q + 4, :].bitcast(I32),
            )
        for h in range(HALVES):
            for g in range(2):
                nc.sync.dma_start(
                    out=w1_raw[:, g, D * h : D * (h + 1)].bitcast(I32),
                    in_=W1_words[g].rearrange("p n t -> p (n t)")[:, PACK * D * h : PACK * D * (h + 1)].bitcast(I32),
                )
        for q in range(4):
            nc.sync.dma_start(
                out=w2_scales[32 * q : 32 * q + 8, :].bitcast(I32),
                in_=W2_scales[:, 4 * q : 4 * q + 4, :].bitcast(I32),
            )
        for g in range(2):
            nc.sync.dma_start(
                out=w2_words[:, g, :].bitcast(I32),
                in_=W2_words[g].rearrange("p n t -> p (n t)").bitcast(I32),
            )

        ident = keep.tile([P, P], F32)
        make_identity(nc, ident[:])
        half = keep.tile([P, POSITIONS + 1], F32)
        nc.vector.memset(half[:], 0.5)
        one = keep.tile([P, POSITIONS + 1], F32)
        nc.vector.memset(one[:], 1.0)
        nc.gpsimd.tensor_copy(out=b1_col[:], in_=b1_bf[:].rearrange("p h t -> p (h t)"))

        def sort_w1_scales(h):
            nc.vector.tensor_copy(
                out=w1_scales[:, h, :, :],
                in_=w1_raw_scales[:, D * h : D * (h + 1)].rearrange("p (m t) -> p t m", t=PACK),
            )

        x_grouped = keep.tile([P, POSITIONS, BATCH, PACK], BF16, align_bytes=64)
        x_grouped_words = x_grouped[:].rearrange("p i b t -> p i (b t)").bitcast(F32).rearrange(
            "p i (b u) -> p i b u", u=2
        )
        x_words = x_sb[:].bitcast(F32)
        rows_b = BATCH // 4
        for a in range(4):
            x_turned = ps_first.tile([P, 2, P], F32, tag="first")
            for u in range(2):
                nc.tensor.transpose(x_turned[:, u, :], x_words[:, a, u : D // 2 : 2], ident[:])
            nc.scalar.copy(
                out=x_grouped_words[:, :, rows_b * a : rows_b * (a + 1), :],
                in_=x_turned[:].rearrange("p u (c i) -> p i c u", i=POSITIONS),
            )
        idle_bank = ps_first.tile([P, D], F32, tag="first")
        for a in range(WARMING_MATMULS):
            nc.tensor.matmul(out=idle_bank[:], lhsT=x_sb[:, a, 0:P], rhs=x_sb[:, a, :], start=True, stop=True)
        xq_words = keep.tile([P, len(X_BLOCKS) * BATCH], U32, align_bytes=64)
        xq_scales = keep.tile([P, len(X_BLOCKS) * BATCH], U8, align_bytes=64)

        def quantise_x(first_block, n_blocks, position):
            cols = slice(BATCH * first_block, BATCH * (first_block + n_blocks))
            nc.vector.quantize_mx(
                out=xq_words[:, cols].bitcast(FP8X4),
                scales=xq_scales[:, cols],
                in_=x_grouped[:, position : position + n_blocks, :, :].rearrange("p i b t -> p (i b t)"),
            )

        def sort_w1(g, h):
            nc.vector.tensor_copy(
                out=w1_words[:, g, h, :, :].bitcast(I32),
                in_=w1_raw[:, g, D * h : D * (h + 1)].bitcast(I32).rearrange("p (m t) -> p t m", t=PACK),
            )

        made = set(range(NATURAL, NATURAL + POSITIONS))

        def quantise_blocks_of(runs):
            for run in runs:
                for first in run:
                    for block in range(first, first + 4, 2):
                        if block in made:
                            continue
                        made.add(block)
                        made.add(block + 1)
                        if X_BLOCKS[block + 1] == X_BLOCKS[block] + 1:
                            quantise_x(block, 2, X_BLOCKS[block])
                        else:
                            quantise_x(block, 1, X_BLOCKS[block])
                            quantise_x(block + 1, 1, X_BLOCKS[block + 1])

        with tc.manual_schedule(engines={mybir.EngineType.DVE}):
            sort_w1_scales(0)
            sort_w1(0, 0)
            sort_w1(1, 0)
            quantise_x(NATURAL, POSITIONS, 0)
            quantise_blocks_of(RUNS[0:2])
            sort_w1_scales(1)
            sort_w1(0, 1)
            sort_w1(1, 1)
            quantise_blocks_of(RUNS[2:])

        n_tiles = 2 * len(RUNS)
        units = [list(range(c, min(c + 4, n_tiles))) for c in range(0, n_tiles, 4)]
        sums = [
            (0, 8, 7, ((0, 6), (1, 7))),
            (8, 14, 13, ((0, 4), (1, 5))),
            (13, 15, None, ((0, 1),)),
            (14, 18, 14, ((0, 2), (1, 3))),
        ]

        p_all = keep.tile([P, n_tiles, D], F32)
        norm2 = keep.tile([P, n_tiles], F32)
        b2_all = keep.tile([P, D], BF16)
        nc.sync.dma_start(out=b2_all[:], in_=b2.partition_broadcast(P))
        gelu_of = {}
        grouped_of = {}
        hq = {}
        second = {}

        def x_slice(block):
            cols = slice(BATCH * block, BATCH * block + 2 * P)
            return xq_words[:, cols].bitcast(FP8X4), xq_scales[:, cols]

        def first_bank(k, t):
            s, h = divmod(k, 2)
            rows = P * len(units[s])
            if t == 0:
                gelu_of[k] = work.tile([P, PACK, PACK * P], BF16, tag="gelu", name="gelu")
            bank = ps_first.tile([P, PACK * P], F32, tag="first")
            for q, c in enumerate(units[s][0::2]):
                for g in range(2):
                    rhs, rhs_scale = x_slice(RUNS[c // 2][g])
                    nc.tensor.matmul_mx(
                        out=bank[:, 2 * P * q : 2 * P * (q + 1)],
                        lhsT=w1_words[:, g, h, t, :].bitcast(FP8X4), lhsT_scale=w1_scales[4 * g : P, h, t, :],
                        rhs=rhs, rhs_scale=rhs_scale,
                        start=(g == 0), stop=(g == 1),
                    )
            nc.scalar.activation(
                out=gelu_of[k][:, t, 0:rows], in_=bank[:, 0:rows], func=ACT.Gelu,
                bias=b1_col[:, PACK * h + t : PACK * h + t + 1],
            )

        def interleave(k):
            rows = P * len(units[k // 2])
            grouped = work.tile([P, PACK * P, PACK], BF16, tag="grouped", align_bytes=64)
            nc.vector.tensor_copy(
                out=grouped[:, 0:rows, :].rearrange("p (c i) t -> p c t i", i=PACK),
                in_=gelu_of[k][:, :, 0:rows].rearrange("p t (c i) -> p c t i", i=PACK),
            )
            grouped_of[k] = grouped

        def quantise(k):
            rows = P * len(units[k // 2])
            words = codes.tile([P, PACK * P], U32, tag="hq_words", align_bytes=64)
            scales = codes.tile([P, PACK * P], U8, tag="hq_scales", align_bytes=64)
            nc.vector.quantize_mx(
                out=words[:, 0:rows].bitcast(FP8X4), scales=scales[:, 0:rows],
                in_=grouped_of[k][:, 0:rows, :].rearrange("p r t -> p (r t)"),
            )
            hq[k] = (words, scales)

        def second_matmul(c):
            s, q = divmod(c, 4)
            acc = ps_second.tile([P, D], F32, tag="second")
            for h in range(HALVES):
                words, scales = hq[2 * s + h]
                rows = slice(P * q, P * (q + 1))
                nc.tensor.matmul_mx(
                    out=acc[:], lhsT=words[:, rows].bitcast(FP8X4), lhsT_scale=scales[:, rows],
                    rhs=w2_words[:, h, :].bitcast(FP8X4), rhs_scale=w2_scales[4 * h : P, :],
                    start=(h == 0), stop=(h == HALVES - 1),
                )
            second[c] = acc

        def add_b2(c):
            nc.vector.tensor_tensor(out=p_all[:, c, :], in0=second[c][:], in1=b2_all[:], op=ALU.add)
            if c == 7:
                nc.sync.dma_start(out=out[:, 0, :], in_=p_all[0:BATCH, c, :])

        def square(c):
            squares = work.tile([P, D], BF16, tag="squares")
            nc.scalar.activation(
                out=squares[:], in_=p_all[:, c, :], func=ACT.Square, scale=0.5, accum_out=norm2[:, c : c + 1]
            )

        norm_of = {}
        shift_of = {}
        tanh_of = {}
        pooled_of = {}
        weight_of = {}

        def norms(e):
            c0, c1, masked, stored = sums[e]
            norm = grp.tile([P, c1 - c0], F32, tag="norm")
            nc.gpsimd.tensor_tensor(out=norm[:], in0=norm2[:, c0:c1], in1=half[:, 0 : c1 - c0], op=ALU.pow)
            norm_of[e] = norm

        def largest(e):
            c0, c1, masked, stored = sums[e]
            norm = norm_of[e]
            if masked is not None:
                nc.vector.memset(norm[0:BATCH, masked - c0 : masked - c0 + 1], -1.0e30)
            shift = grp.tile([P, 1], F32, tag="shift")
            nc.vector.reduce_max(out=shift[:], in_=norm[:], axis=AX.X, negate=True)
            shift_of[e] = shift

        def shifted_tanh(e):
            c0, c1, masked, stored = sums[e]
            th = grp.tile([P, c1 - c0], F32, tag="th")
            nc.scalar.activation(out=th[:], in_=norm_of[e][:], func=ACT.Tanh, bias=shift_of[e][:])
            tanh_of[e] = th

        def weights(e):
            c0, c1, masked, stored = sums[e]
            n = c1 - c0
            th = tanh_of[e]
            den = grp.tile([P, n], F32, tag="den")
            nc.vector.tensor_scalar(den[:], th[:], -1.0, 1.0, ALU.mult, ALU.add)
            nc.vector.reciprocal(den[:], den[:])
            ex = grp.tile([P, n], F32, tag="ex")
            total = grp.tile([P, 1], F32, tag="total")
            nc.vector.scalar_tensor_tensor(
                out=ex[:], in0=den[:], scalar=2.0, in1=one[:, 0:n], op0=ALU.mult, op1=ALU.subtract, accum_out=total[:]
            )
            nc.vector.reciprocal(total[:], total[:])
            weight = grp.tile([P, n], F32, tag="weight")
            nc.vector.tensor_scalar(weight[:], ex[:], total[:], None, ALU.mult)
            weight_of[e] = weight

        def pool_tile(e, c):
            c0, c1, masked, stored = sums[e]
            w = weight_of[e][:, c - c0 : c - c0 + 1]
            if c == c0:
                pooled_of[e] = grp.tile([P, D], F32, tag="pooled", name="pooled")
                nc.vector.tensor_scalar(pooled_of[e][:], p_all[:, c, :], w, None, ALU.mult)
            else:
                nc.vector.scalar_tensor_tensor(
                    out=pooled_of[e][:], in0=p_all[:, c, :], scalar=w, in1=pooled_of[e][:], op0=ALU.mult, op1=ALU.add
                )
            if c == c1 - 1:
                for s, i in stored:
                    nc.sync.dma_start(out=out[:, i, :], in_=pooled_of[e][BATCH * s : BATCH * (s + 1), :])

        n_first = 2 * len(units)
        second_at = {}
        for s, unit in enumerate(units):
            second_at.setdefault(2 * s + 3, []).extend(unit[0:2])
            second_at.setdefault(2 * s + 4, []).extend(unit[2:4])
        last_of = {sums[e][1] - 1: e for e in range(len(sums))}

        to_square = []
        to_norm = []
        to_max = []
        to_weigh = []
        waiting = []
        step = 0
        finished = 0
        while finished < len(sums) or waiting:
            running = step < n_first
            arrived = second_at.get(step, [])
            for c in arrived:
                second_matmul(c)
            for c in to_square:
                square(c)
                if c in last_of:
                    to_norm.append(last_of[c])
            to_square = []
            for e in to_norm:
                norms(e)
                to_max.append(e)
            to_norm = []
            if 0 <= step - 1 < n_first:
                interleave(step - 1)
            for e in to_weigh:
                weights(e)
                waiting.extend([(e, c) for c in range(sums[e][0], sums[e][1])])
                finished += 1
            to_weigh = []
            if arrived:
                add_b2(arrived[0])
            if 0 <= step - 1 < n_first:
                quantise(step - 1)
            for c in arrived[1:]:
                add_b2(c)
            to_square.extend(arrived)
            for e in to_max:
                largest(e)
            for t in range(PACK):
                if running:
                    first_bank(step, t)
                if t == 1:
                    for e in to_max:
                        shifted_tanh(e)
                        to_weigh.append(e)
                    to_max = []
            quota = POOLED_PER_STEP
            for e, c in waiting[0:quota]:
                pool_tile(e, c)
            waiting = waiting[quota:]
            step += 1
